import numpy as np
import ml_dtypes


def mxq(x, axis, fmt="e4m3"):
    dtype, down = {"e4m3": (ml_dtypes.float8_e4m3fn, 7), "e5m2": (ml_dtypes.float8_e5m2, 14)}[fmt]
    v = np.moveaxis(np.asarray(x, np.float32).astype(ml_dtypes.bfloat16).astype(np.float64), axis, -1)
    blocks = v.reshape(v.shape[:-1] + (-1, 32))
    amax = np.abs(blocks).max(-1, keepdims=True)
    byte = np.maximum(np.where(amax > 0, np.frexp(amax)[1] - 1 + 127, 0) - down, 1)
    scale = np.exp2(byte - 127.0)
    codes = (blocks / scale).astype(np.float32).astype(dtype).astype(np.float64)
    return np.moveaxis((codes * scale).reshape(v.shape), -1, axis)


WIDE = False


def mx_kscale(k):
    if not WIDE:
        return np.ones(k)
    levels = np.array([10, -10, 5, -5, 0])
    a = np.random.permutation(np.resize(levels, k // 512 * 4)).reshape(k // 512, 4)
    idx = np.arange(k)
    return np.exp2(a[idx // 512, idx % 128 // 32])


BF16 = ml_dtypes.bfloat16


def bf(x):
    return np.asarray(x, np.float32).astype(BF16)


def f64(x):
    return np.asarray(x).astype(np.float64)


L, P, B, H = 4, 2, 4096, 512
KEEP_PROB = 0.7


def setup_inputs():
    s = mx_kscale(H)
    w = np.random.standard_normal((P, H, H)) / np.sqrt(H)
    w[0] = w[0] / s[None, :]
    return {"h_in": bf(np.random.standard_normal((B, H)) * 1.3 * s),
            "w": bf(w),
            "masks": bf(np.random.uniform(size=(P, H, H)) < KEEP_PROB),
            "mu": bf(np.random.uniform(-0.5, 0.5, (P, H))),
            "sigma": bf(np.random.uniform(0.05, 0.5, (P, H))),
            "z": bf(np.random.standard_normal((P, B, H)))}


def reference(h_in, w, masks, mu, sigma, z):
    h, w, masks, mu, sigma, z = f64(h_in), f64(w), f64(masks), f64(mu), f64(sigma), f64(z)
    acts = []
    for l in range(P):
        wm_t = (w[l] * masks[l]).T
        pre = mxq(h, 1, "e4m3") @ mxq(wm_t, 0, "e4m3")
        noise = np.exp(mu[l][None, :] + sigma[l][None, :] * z[l])
        h = np.maximum(pre + noise, 0.0)
        acts.append(h)
    return np.concatenate(acts, axis=1)

@@ -1,0 +1,289 @@
+from contextlib import ExitStack
+
+import concourse.mybir as mybir
+from concourse.masks import make_identity
+
+FLOPS = 2 * 2 * 4096 * 512 * 512
+
+F32 = mybir.dt.float32
+BF16 = mybir.dt.bfloat16
+U32 = mybir.dt.uint32
+U8 = mybir.dt.uint8
+FP8X4 = mybir.dt.float8_e4m3fn_x4
+ACT = mybir.ActivationFunctionType
+ALU = mybir.AluOpType
+
+P = 128
+PACK = 4
+FEATURES = P * PACK
+LAYERS = 2
+ROWS = 4096
+CHUNK = 512
+CHUNKS = ROWS // CHUNK
+ROW_TILES = CHUNK // P
+BLOCKS = FEATURES // P
+WORDS = FEATURES // 2
+FLOAT_MAX = 3.4028234663852886e38
+
+LOAD_AHEAD = 6
+SCALAR_ROW_TILES = 3
+
+
+def unit_order():
+    units = []
+    for chunk in range(CHUNKS + 1):
+        if chunk < CHUNKS:
+            units.append((chunk, 0))
+        if chunk >= 1:
+            units.append((chunk - 1, 1))
+    return units
+
+
+def tile_scm_mlp_pa_t_kernel(tc, h_in, w, masks, mu, sigma, z, out):
+    nc = tc.nc
+    units = unit_order()
+    n_units = len(units)
+
+    def unit_at(i):
+        return units[i] if 0 <= i < n_units else None
+
+    with ExitStack() as ctx:
+        const = ctx.enter_context(tc.tile_pool(name="const", bufs=1))
+        weights = ctx.enter_context(tc.tile_pool(name="weights", bufs=1))
+        h_pool = ctx.enter_context(tc.tile_pool(name="h_pool", bufs=4))
+        z_pool = ctx.enter_context(tc.tile_pool(name="z_pool", bufs=LOAD_AHEAD + 1))
+        sum_pool = ctx.enter_context(tc.tile_pool(name="sum_pool", bufs=4))
+        group_pool = ctx.enter_context(tc.tile_pool(name="group_pool", bufs=2))
+        code_pool = ctx.enter_context(tc.tile_pool(name="code_pool", bufs=2))
+        out_pool = ctx.enter_context(tc.tile_pool(name="out_pool", bufs=3))
+        psum_pre = ctx.enter_context(tc.psum_pool(name="psum_pre", bufs=3))
+        psum_tr = ctx.enter_context(tc.psum_pool(name="psum_tr", bufs=5))
+        ctx.enter_context(tc.manual_schedule())
+
+        h_sb = {}
+        z_sb = {}
+        w_sb = {}
+        m_sb = {}
+        w_grouped = {}
+        w_codes = {}
+        w_scales = {}
+        h_grouped = {}
+        a_grouped = {}
+        x_codes = {}
+        x_scales = {}
+        sums = {}
+        out_sb = {}
+
+        def load_rows(pool, src, chunk, name):
+            rows = pool.tile([P, ROW_TILES * FEATURES], BF16, name=name, tag=name)
+            nc.sync.dma_start(
+                out=rows[:],
+                in_=src[chunk * CHUNK : (chunk + 1) * CHUNK, :].rearrange(
+                    "(p j) k -> p (j k)", j=ROW_TILES
+                ),
+            )
+            return rows
+
+        def load_unit(unit):
+            chunk, layer = unit
+            if layer == 0:
+                h_sb[chunk] = load_rows(h_pool, h_in, chunk, "h_rows")
+            z_sb[unit] = load_rows(z_pool, z[layer], chunk, "z_rows")
+
+        def load_weights(layer):
+            for src, store, name in ((w, w_sb, "w_raw%d"), (masks, m_sb, "m_raw%d")):
+                raw = weights.tile([P, BLOCKS, FEATURES], BF16, name=name % layer)
+                nc.sync.dma_start(
+                    out=raw[:].rearrange("q (u e) k -> q u (e k)", e=2),
+                    in_=src[layer].rearrange("(u q e) k -> q u (e k)", u=2, e=2),
+                )
+                store[layer] = raw
+
+        ident_f32 = const.tile([P, P], F32)
+        make_identity(nc, ident_f32[:])
+        ident_bf16 = const.tile([P, P], BF16)
+        make_identity(nc, ident_bf16[:])
+
+        noise_scale = const.tile([P, LAYERS, BLOCKS], F32)
+        noise_bias = const.tile([P, LAYERS, BLOCKS], F32)
+        with nc.allow_non_contiguous_dma(reason="two small vectors, two features to a partition"):
+            for layer in range(LAYERS):
+                for src, dst, name in ((sigma, noise_scale, "sg%d"), (mu, noise_bias, "mu%d")):
+                    raw = const.tile([P, BLOCKS], BF16, name=name % layer)
+                    nc.scalar.dma_start(
+                        out=raw[:].rearrange("q (u e) -> q u e", e=2),
+                        in_=src[layer].rearrange("(u q e) -> q u e", u=2, e=2),
+                    )
+                    nc.vector.tensor_copy(out=dst[:, layer, :], in_=raw[:])
+
+        def mask_weights(layer):
+            nc.vector.tensor_tensor(
+                out=w_sb[layer][:], in0=w_sb[layer][:], in1=m_sb[layer][:], op=ALU.mult
+            )
+
+        def transpose_weights(layer):
+            grouped = weights.tile([P, FEATURES, PACK], BF16, name="w_grouped%d" % layer, align_bytes=64)
+            for pair in range(BLOCKS // 2):
+                w_t = psum_tr.tile([P, 2, PACK, P], BF16, name="w_t", tag="tr")
+                for bb in range(2):
+                    k_view = w_sb[layer][:, 2 * pair + bb, :].rearrange(
+                        "q (u p e) -> q u e p", u=2, e=2
+                    )
+                    for t in range(PACK):
+                        nc.tensor.transpose(w_t[:, bb, t, :], k_view[:, t // 2, t % 2, :], ident_bf16[:])
+                dst = grouped[:, 2 * pair * P : (2 * pair + 2) * P, :].rearrange(
+                    "p (bb q) t -> p bb q t", bb=2
+                )
+                if pair == 0:
+                    nc.scalar.copy(out=dst, in_=w_t[:].rearrange("p bb t q -> p bb q t"))
+                else:
+                    nc.vector.tensor_copy(out=dst, in_=w_t[:].rearrange("p bb t q -> p bb q t"))
+            w_grouped[layer] = grouped
+
+        def quantise_weights(layer):
+            w_codes[layer] = weights.tile([P, FEATURES], U32, name="w_codes%d" % layer, align_bytes=64)
+            w_scales[layer] = weights.tile([P, FEATURES], U8, name="w_scales%d" % layer, align_bytes=64)
+            nc.vector.quantize_mx(
+                out=w_codes[layer][:].bitcast(FP8X4),
+                scales=w_scales[layer][:],
+                in_=w_grouped[layer][:].rearrange("p c t -> p (c t)"),
+            )
+
+        def transpose_h(chunk):
+            words = h_sb[chunk][:].bitcast(F32)
+            grouped = group_pool.tile([P, CHUNK * PACK], BF16, name="h_grouped", tag="h_grouped", align_bytes=64)
+            grouped_words = grouped[:].bitcast(F32).rearrange("p (c u) -> p c u", u=2)
+            for half in range(ROW_TILES // 2):
+                h_t = psum_tr.tile([P, 2, 2 * P], F32, name="h_t", tag="tr")
+                for jj in range(2):
+                    j = 2 * half + jj
+                    for u in range(2):
+                        nc.tensor.transpose(
+                            h_t[:, u, jj * P : (jj + 1) * P],
+                            words[:, j * WORDS + u * P : j * WORDS + (u + 1) * P],
+                            ident_f32[:],
+                        )
+                nc.vector.tensor_copy(
+                    out=grouped_words[:, 2 * half * P : (2 * half + 2) * P, :],
+                    in_=h_t[:].rearrange("p u c -> p c u"),
+                )
+            h_grouped[chunk] = grouped
+
+        def quantise_moving(unit, grouped_flat, name):
+            x_codes[unit] = code_pool.tile([P, CHUNK], U32, name=name + "_codes", tag=name + "_codes", align_bytes=64)
+            x_scales[unit] = code_pool.tile([P, CHUNK], U8, name=name + "_scales", tag=name + "_scales", align_bytes=64)
+            nc.vector.quantize_mx(
+                out=x_codes[unit][:].bitcast(FP8X4), scales=x_scales[unit][:], in_=grouped_flat
+            )
+
+        def noise(unit):
+            chunk, layer = unit
+            words = z_sb[unit][:].bitcast(F32)
+            total = sum_pool.tile([P, BLOCKS, CHUNK], F32, name="total", tag="total")
+            for u in range(2):
+                z_t = psum_tr.tile([P, CHUNK], F32, name="z_t", tag="tr")
+                for j in range(ROW_TILES):
+                    nc.tensor.transpose(
+                        z_t[:, j * P : (j + 1) * P],
+                        words[:, j * WORDS + u * P : j * WORDS + (u + 1) * P],
+                        ident_f32[:],
+                    )
+                pairs = z_t[:].bitcast(BF16).rearrange("q (c e) -> q c e", e=2)
+                for e in range(2):
+                    b = 2 * u + e
+                    nc.scalar.activation(
+                        out=total[:, b, :],
+                        in_=pairs[:, :, e],
+                        func=ACT.Exp,
+                        bias=noise_bias[:, layer, b : b + 1],
+                        scale=noise_scale[:, layer, b : b + 1],
+                    )
+            sums[unit] = total
+
+        def multiply_and_add(unit):
+            chunk, layer = unit
+            total = sums[unit]
+            pre = []
+            for b in range(BLOCKS):
+                acc = psum_pre.tile([P, CHUNK], F32, name="acc", tag="acc")
+                nc.tensor.matmul_mx(
+                    out=acc[:],
+                    lhsT=w_codes[layer][:, b * P : (b + 1) * P].bitcast(FP8X4),
+                    lhsT_scale=w_scales[layer][:, b * P : (b + 1) * P],
+                    rhs=x_codes[unit][:].bitcast(FP8X4),
+                    rhs_scale=x_scales[unit][:],
+                    start=True,
+                    stop=True,
+                )
+                pre.append(acc)
+            for b in range(BLOCKS):
+                nc.vector.tensor_tensor(out=total[:, b, :], in0=pre[b][:], in1=total[:, b, :], op=ALU.add)
+            if layer == 0:
+                grouped = group_pool.tile([P, CHUNK, PACK], BF16, name="a_grouped", tag="a_grouped", align_bytes=64)
+                nc.gpsimd.tensor_scalar(
+                    out=grouped[:],
+                    in0=total[:].rearrange("q b c -> q c b"),
+                    scalar1=FLOAT_MAX,
+                    scalar2=0.0,
+                    op0=ALU.min,
+                    op1=ALU.max,
+                )
+                a_grouped[chunk] = grouped
+
+        def finish(unit):
+            chunk, layer = unit
+            total = sums[unit]
+            if layer == 0:
+                out_sb[chunk] = out_pool.tile([P, ROW_TILES, LAYERS * FEATURES], F32, name="out_rows", tag="out_rows")
+            rows = out_sb[chunk]
+            dram = out[chunk * CHUNK : (chunk + 1) * CHUNK, :].rearrange("(p j) f -> p j f", j=ROW_TILES)
+            for j in range(ROW_TILES):
+                o_t = psum_tr.tile([P, BLOCKS, P], F32, name="o_t", tag="tr")
+                for b in range(BLOCKS):
+                    nc.tensor.transpose(o_t[:, b, :], total[:, b, j * P : (j + 1) * P], ident_f32[:])
+                dst = rows[:, j, layer * FEATURES : (layer + 1) * FEATURES].rearrange(
+                    "p (u q e) -> p u q e", u=2, e=2
+                )
+                src = o_t[:].rearrange("p (u e) q -> p u q e", e=2)
+                if j < SCALAR_ROW_TILES:
+                    nc.scalar.activation(out=dst, in_=src, func=ACT.Relu)
+                else:
+                    nc.vector.tensor_scalar_max(out=dst, in0=src, scalar1=0.0)
+                if layer == LAYERS - 1 and j % 2 == 1:
+                    nc.sync.dma_start(out=dram[:, j - 1 : j + 1, :], in_=rows[:, j - 1 : j + 1, :])
+
+        first_use = [units.index((0, layer)) for layer in range(LAYERS)]
+
+        load_weights(0)
+        load_unit(units[0])
+        load_unit(units[1])
+        load_weights(1)
+        load_unit(units[2])
+
+        for n in range(-3, n_units + 1):
+            ahead = unit_at(n + LOAD_AHEAD)
+            if ahead is not None and n + LOAD_AHEAD >= 3:
+                load_unit(ahead)
+
+            if unit_at(n) is not None:
+                multiply_and_add(unit_at(n))
+            if unit_at(n - 1) is not None:
+                finish(unit_at(n - 1))
+            if unit_at(n + 1) is not None:
+                noise(unit_at(n + 1))
+            two_ahead = unit_at(n + 2)
+            if two_ahead is not None and two_ahead[1] == 0:
+                transpose_h(two_ahead[0])
+            one_ahead = unit_at(n + 1)
+            if one_ahead is not None and one_ahead[1] == 0:
+                quantise_moving(one_ahead, h_grouped[one_ahead[0]][:], "h")
+            behind = unit_at(n - 1)
+            if behind is not None and behind[1] == 0:
+                quantise_moving((behind[0], 1), a_grouped[behind[0]][:].rearrange("p c t -> p (c t)"), "a")
+            for layer in range(LAYERS):
+                if n == first_use[layer] - 3:
+                    mask_weights(layer)
+                if n == first_use[layer] - 2:
+                    transpose_weights(layer)
+                if n == first_use[layer] - 1:
+                    quantise_weights(layer)

@@ -22,20 +22,22 @@ CHUNK = 512
 CHUNKS = ROWS // CHUNK
 ROW_TILES = CHUNK // P
 BLOCKS = FEATURES // P
+HALVES = 2
 WORDS = FEATURES // 2
 FLOAT_MAX = 3.4028234663852886e38
 
+LAYER_LAG = 2
 LOAD_AHEAD = 6
-SCALAR_ROW_TILES = 3
+FRONT_AHEAD = 2
 
 
 def unit_order():
     units = []
-    for chunk in range(CHUNKS + 1):
+    for chunk in range(CHUNKS + LAYER_LAG):
         if chunk < CHUNKS:
             units.append((chunk, 0))
-        if chunk >= 1:
-            units.append((chunk - 1, 1))
+        if chunk >= LAYER_LAG:
+            units.append((chunk - LAYER_LAG, 1))
     return units
 
 
@@ -47,15 +49,19 @@ def tile_scm_mlp_pa_t_kernel(tc, h_in, w, masks, mu, sigma, z, out):
     def unit_at(i):
         return units[i] if 0 <= i < n_units else None
 
+    def layer_at(i):
+        return units[i][1] if 0 <= i < n_units else None
+
     with ExitStack() as ctx:
         const = ctx.enter_context(tc.tile_pool(name="const", bufs=1))
         weights = ctx.enter_context(tc.tile_pool(name="weights", bufs=1))
         h_pool = ctx.enter_context(tc.tile_pool(name="h_pool", bufs=4))
-        z_pool = ctx.enter_context(tc.tile_pool(name="z_pool", bufs=LOAD_AHEAD + 1))
-        sum_pool = ctx.enter_context(tc.tile_pool(name="sum_pool", bufs=4))
-        group_pool = ctx.enter_context(tc.tile_pool(name="group_pool", bufs=2))
-        code_pool = ctx.enter_context(tc.tile_pool(name="code_pool", bufs=2))
-        out_pool = ctx.enter_context(tc.tile_pool(name="out_pool", bufs=3))
+        z_pool = ctx.enter_context(tc.tile_pool(name="z_pool", bufs=LOAD_AHEAD))
+        sum_pool = ctx.enter_context(tc.tile_pool(name="sum_pool", bufs=7))
+        h_group_pool = ctx.enter_context(tc.tile_pool(name="h_group_pool", bufs=2))
+        a_group_pool = ctx.enter_context(tc.tile_pool(name="a_group_pool", bufs=3))
+        code_pool = ctx.enter_context(tc.tile_pool(name="code_pool", bufs=3))
+        out_pool = ctx.enter_context(tc.tile_pool(name="out_pool", bufs=4))
         psum_pre = ctx.enter_context(tc.psum_pool(name="psum_pre", bufs=3))
         psum_tr = ctx.enter_context(tc.psum_pool(name="psum_tr", bufs=5))
         ctx.enter_context(tc.manual_schedule())
@@ -72,6 +78,7 @@ def tile_scm_mlp_pa_t_kernel(tc, h_in, w, masks, mu, sigma, z, out):
         x_codes = {}
         x_scales = {}
         sums = {}
+        accs = {}
         out_sb = {}
 
         def load_rows(pool, src, chunk, name):
@@ -91,13 +98,16 @@ def tile_scm_mlp_pa_t_kernel(tc, h_in, w, masks, mu, sigma, z, out):
             z_sb[unit] = load_rows(z_pool, z[layer], chunk, "z_rows")
 
         def load_weights(layer):
-            for src, store, name in ((w, w_sb, "w_raw%d"), (masks, m_sb, "m_raw%d")):
-                raw = weights.tile([P, BLOCKS, FEATURES], BF16, name=name % layer)
-                nc.sync.dma_start(
-                    out=raw[:].rearrange("q (u e) k -> q u (e k)", e=2),
-                    in_=src[layer].rearrange("(u q e) k -> q u (e k)", u=2, e=2),
-                )
-                store[layer] = raw
+            w_sb[layer] = weights.tile([P, BLOCKS, FEATURES], BF16, name="w_raw%d" % layer)
+            m_sb[layer] = weights.tile([P, BLOCKS, FEATURES], BF16, name="m_raw%d" % layer)
+            for half in range(HALVES):
+                for src, raw in ((w, w_sb[layer]), (masks, m_sb[layer])):
+                    nc.sync.dma_start(
+                        out=raw[:, 2 * half : 2 * half + 2, :].rearrange("q e k -> q (e k)"),
+                        in_=src[layer][2 * half * P : (2 * half + 2) * P, :].rearrange(
+                            "(q e) k -> q (e k)", e=2
+                        ),
+                    )
 
         ident_f32 = const.tile([P, P], F32)
         make_identity(nc, ident_f32[:])
@@ -117,24 +127,29 @@ def tile_scm_mlp_pa_t_kernel(tc, h_in, w, masks, mu, sigma, z, out):
                     nc.vector.tensor_copy(out=dst[:, layer, :], in_=raw[:])
 
         def mask_weights(layer):
-            nc.vector.tensor_tensor(
-                out=w_sb[layer][:], in0=w_sb[layer][:], in1=m_sb[layer][:], op=ALU.mult
-            )
+            for half in range(HALVES):
+                blocks = slice(2 * half, 2 * half + 2)
+                nc.vector.tensor_tensor(
+                    out=w_sb[layer][:, blocks, :],
+                    in0=w_sb[layer][:, blocks, :],
+                    in1=m_sb[layer][:, blocks, :],
+                    op=ALU.mult,
+                )
 
         def transpose_weights(layer):
             grouped = weights.tile([P, FEATURES, PACK], BF16, name="w_grouped%d" % layer, align_bytes=64)
-            for pair in range(BLOCKS // 2):
+            for half in range(HALVES):
                 w_t = psum_tr.tile([P, 2, PACK, P], BF16, name="w_t", tag="tr")
                 for bb in range(2):
-                    k_view = w_sb[layer][:, 2 * pair + bb, :].rearrange(
+                    k_view = w_sb[layer][:, 2 * half + bb, :].rearrange(
                         "q (u p e) -> q u e p", u=2, e=2
                     )
                     for t in range(PACK):
                         nc.tensor.transpose(w_t[:, bb, t, :], k_view[:, t // 2, t % 2, :], ident_bf16[:])
-                dst = grouped[:, 2 * pair * P : (2 * pair + 2) * P, :].rearrange(
+                dst = grouped[:, 2 * half * P : (2 * half + 2) * P, :].rearrange(
                     "p (bb q) t -> p bb q t", bb=2
                 )
-                if pair == 0:
+                if half == 0:
                     nc.scalar.copy(out=dst, in_=w_t[:].rearrange("p bb t q -> p bb q t"))
                 else:
                     nc.vector.tensor_copy(out=dst, in_=w_t[:].rearrange("p bb t q -> p bb q t"))
@@ -143,17 +158,19 @@ def tile_scm_mlp_pa_t_kernel(tc, h_in, w, masks, mu, sigma, z, out):
         def quantise_weights(layer):
             w_codes[layer] = weights.tile([P, FEATURES], U32, name="w_codes%d" % layer, align_bytes=64)
             w_scales[layer] = weights.tile([P, FEATURES], U8, name="w_scales%d" % layer, align_bytes=64)
-            nc.vector.quantize_mx(
-                out=w_codes[layer][:].bitcast(FP8X4),
-                scales=w_scales[layer][:],
-                in_=w_grouped[layer][:].rearrange("p c t -> p (c t)"),
-            )
+            for half in range(HALVES):
+                cols = slice(2 * half * P, (2 * half + 2) * P)
+                nc.vector.quantize_mx(
+                    out=w_codes[layer][:, cols].bitcast(FP8X4),
+                    scales=w_scales[layer][:, cols],
+                    in_=w_grouped[layer][:, cols, :].rearrange("p c t -> p (c t)"),
+                )
 
         def transpose_h(chunk):
             words = h_sb[chunk][:].bitcast(F32)
-            grouped = group_pool.tile([P, CHUNK * PACK], BF16, name="h_grouped", tag="h_grouped", align_bytes=64)
+            grouped = h_group_pool.tile([P, CHUNK * PACK], BF16, name="h_grouped", tag="h_grouped", align_bytes=64)
             grouped_words = grouped[:].bitcast(F32).rearrange("p (c u) -> p c u", u=2)
-            for half in range(ROW_TILES // 2):
+            for half in range(HALVES):
                 h_t = psum_tr.tile([P, 2, 2 * P], F32, name="h_t", tag="tr")
                 for jj in range(2):
                     j = 2 * half + jj
@@ -163,7 +180,7 @@ def tile_scm_mlp_pa_t_kernel(tc, h_in, w, masks, mu, sigma, z, out):
                             words[:, j * WORDS + u * P : j * WORDS + (u + 1) * P],
                             ident_f32[:],
                         )
-                nc.vector.tensor_copy(
+                nc.scalar.copy(
                     out=grouped_words[:, 2 * half * P : (2 * half + 2) * P, :],
                     in_=h_t[:].rearrange("p u c -> p c u"),
                 )
@@ -176,35 +193,34 @@ def tile_scm_mlp_pa_t_kernel(tc, h_in, w, masks, mu, sigma, z, out):
                 out=x_codes[unit][:].bitcast(FP8X4), scales=x_scales[unit][:], in_=grouped_flat
             )
 
-        def noise(unit):
+        def noise(unit, u):
             chunk, layer = unit
             words = z_sb[unit][:].bitcast(F32)
-            total = sum_pool.tile([P, BLOCKS, CHUNK], F32, name="total", tag="total")
-            for u in range(2):
-                z_t = psum_tr.tile([P, CHUNK], F32, name="z_t", tag="tr")
-                for j in range(ROW_TILES):
-                    nc.tensor.transpose(
-                        z_t[:, j * P : (j + 1) * P],
-                        words[:, j * WORDS + u * P : j * WORDS + (u + 1) * P],
-                        ident_f32[:],
-                    )
-                pairs = z_t[:].bitcast(BF16).rearrange("q (c e) -> q c e", e=2)
-                for e in range(2):
-                    b = 2 * u + e
-                    nc.scalar.activation(
-                        out=total[:, b, :],
-                        in_=pairs[:, :, e],
-                        func=ACT.Exp,
-                        bias=noise_bias[:, layer, b : b + 1],
-                        scale=noise_scale[:, layer, b : b + 1],
-                    )
-            sums[unit] = total
+            if u == 0:
+                sums[unit] = sum_pool.tile([P, BLOCKS, CHUNK], F32, name="total", tag="total")
+            total = sums[unit]
+            z_t = psum_tr.tile([P, CHUNK], F32, name="z_t", tag="tr")
+            for j in range(ROW_TILES):
+                nc.tensor.transpose(
+                    z_t[:, j * P : (j + 1) * P],
+                    words[:, j * WORDS + u * P : j * WORDS + (u + 1) * P],
+                    ident_f32[:],
+                )
+            pairs = z_t[:].bitcast(BF16).rearrange("q (c e) -> q c e", e=2)
+            for e in range(2):
+                b = 2 * u + e
+                nc.scalar.activation(
+                    out=total[:, b, :],
+                    in_=pairs[:, :, e],
+                    func=ACT.Exp,
+                    bias=noise_bias[:, layer, b : b + 1],
+                    scale=noise_scale[:, layer, b : b + 1],
+                )
 
-        def multiply_and_add(unit):
+        def multiply_and_add(unit, half):
             chunk, layer = unit
             total = sums[unit]
-            pre = []
-            for b in range(BLOCKS):
+            for b in range(2 * half, 2 * half + 2):
                 acc = psum_pre.tile([P, CHUNK], F32, name="acc", tag="acc")
                 nc.tensor.matmul_mx(
                     out=acc[:],
@@ -215,75 +231,89 @@ def tile_scm_mlp_pa_t_kernel(tc, h_in, w, masks, mu, sigma, z, out):
                     start=True,
                     stop=True,
                 )
-                pre.append(acc)
-            for b in range(BLOCKS):
-                nc.vector.tensor_tensor(out=total[:, b, :], in0=pre[b][:], in1=total[:, b, :], op=ALU.add)
-            if layer == 0:
-                grouped = group_pool.tile([P, CHUNK, PACK], BF16, name="a_grouped", tag="a_grouped", align_bytes=64)
-                nc.gpsimd.tensor_scalar(
-                    out=grouped[:],
-                    in0=total[:].rearrange("q b c -> q c b"),
-                    scalar1=FLOAT_MAX,
-                    scalar2=0.0,
-                    op0=ALU.min,
-                    op1=ALU.max,
-                )
-                a_grouped[chunk] = grouped
+                accs[b] = acc
+            for b in range(2 * half, 2 * half + 2):
+                nc.vector.tensor_tensor(out=total[:, b, :], in0=accs[b][:], in1=total[:, b, :], op=ALU.add)
 
-        def finish(unit):
+        def regroup_a0(chunk):
+            grouped = a_group_pool.tile([P, CHUNK, PACK], BF16, name="a_grouped", tag="a_grouped", align_bytes=64)
+            nc.gpsimd.tensor_scalar(
+                out=grouped[:],
+                in0=sums[(chunk, 0)][:].rearrange("q b c -> q c b"),
+                scalar1=FLOAT_MAX,
+                scalar2=0.0,
+                op0=ALU.min,
+                op1=ALU.max,
+            )
+            a_grouped[chunk] = grouped
+
+        def finish(unit, half):
             chunk, layer = unit
             total = sums[unit]
-            if layer == 0:
-                out_sb[chunk] = out_pool.tile([P, ROW_TILES, LAYERS * FEATURES], F32, name="out_rows", tag="out_rows")
-            rows = out_sb[chunk]
-            dram = out[chunk * CHUNK : (chunk + 1) * CHUNK, :].rearrange("(p j) f -> p j f", j=ROW_TILES)
-            for j in range(ROW_TILES):
+            if half == 0:
+                out_sb[unit] = out_pool.tile([P, ROW_TILES, FEATURES], F32, name="out_rows", tag="out_rows")
+            rows = out_sb[unit]
+            for j in range(2 * half, 2 * half + 2):
                 o_t = psum_tr.tile([P, BLOCKS, P], F32, name="o_t", tag="tr")
                 for b in range(BLOCKS):
                     nc.tensor.transpose(o_t[:, b, :], total[:, b, j * P : (j + 1) * P], ident_f32[:])
-                dst = rows[:, j, layer * FEATURES : (layer + 1) * FEATURES].rearrange(
-                    "p (u q e) -> p u q e", u=2, e=2
-                )
+                dst = rows[:, j, :].rearrange("p (u q e) -> p u q e", u=2, e=2)
                 src = o_t[:].rearrange("p (u e) q -> p u q e", e=2)
-                if j < SCALAR_ROW_TILES:
+                if j % 2 == 0:
                     nc.scalar.activation(out=dst, in_=src, func=ACT.Relu)
                 else:
                     nc.vector.tensor_scalar_max(out=dst, in0=src, scalar1=0.0)
-                if layer == LAYERS - 1 and j % 2 == 1:
-                    nc.sync.dma_start(out=dram[:, j - 1 : j + 1, :], in_=rows[:, j - 1 : j + 1, :])
+            dram = out[
+                chunk * CHUNK : (chunk + 1) * CHUNK, layer * FEATURES : (layer + 1) * FEATURES
+            ].rearrange("(p j) f -> p j f", j=ROW_TILES)
+            nc.sync.dma_start(
+                out=dram[:, 2 * half : 2 * half + 2, :], in_=rows[:, 2 * half : 2 * half + 2, :]
+            )
 
-        first_use = [units.index((0, layer)) for layer in range(LAYERS)]
+        first_layer1 = units.index((0, 1))
 
         load_weights(0)
-        load_unit(units[0])
-        load_unit(units[1])
-        load_weights(1)
-        load_unit(units[2])
+        for i in range(LOAD_AHEAD):
+            if i == first_layer1:
+                load_weights(1)
+            load_unit(units[i])
 
-        for n in range(-3, n_units + 1):
-            ahead = unit_at(n + LOAD_AHEAD)
-            if ahead is not None and n + LOAD_AHEAD >= 3:
-                load_unit(ahead)
+        mask_weights(0)
+        transpose_weights(0)
+        quantise_weights(0)
+        for i in range(FRONT_AHEAD):
+            transpose_h(units[i][0])
+            if i == 0:
+                quantise_moving(units[i], h_grouped[units[i][0]][:], "h")
+            for u in range(HALVES):
+                noise(units[i], u)
 
-            if unit_at(n) is not None:
-                multiply_and_add(unit_at(n))
-            if unit_at(n - 1) is not None:
-                finish(unit_at(n - 1))
-            if unit_at(n + 1) is not None:
-                noise(unit_at(n + 1))
-            two_ahead = unit_at(n + 2)
-            if two_ahead is not None and two_ahead[1] == 0:
-                transpose_h(two_ahead[0])
-            one_ahead = unit_at(n + 1)
-            if one_ahead is not None and one_ahead[1] == 0:
-                quantise_moving(one_ahead, h_grouped[one_ahead[0]][:], "h")
-            behind = unit_at(n - 1)
-            if behind is not None and behind[1] == 0:
-                quantise_moving((behind[0], 1), a_grouped[behind[0]][:].rearrange("p c t -> p (c t)"), "a")
-            for layer in range(LAYERS):
-                if n == first_use[layer] - 3:
-                    mask_weights(layer)
-                if n == first_use[layer] - 2:
-                    transpose_weights(layer)
-                if n == first_use[layer] - 1:
-                    quantise_weights(layer)
+        for n in range(n_units + 1):
+            if unit_at(n + LOAD_AHEAD) is not None:
+                load_unit(unit_at(n + LOAD_AHEAD))
+
+            for half in range(HALVES):
+                if unit_at(n) is not None:
+                    multiply_and_add(unit_at(n), half)
+                    if half == HALVES - 1 and layer_at(n) == 0:
+                        regroup_a0(unit_at(n)[0])
+                if unit_at(n - 1) is not None:
+                    finish(unit_at(n - 1), half)
+                if half == 0:
+                    if layer_at(n + 1) == 0:
+                        quantise_moving(unit_at(n + 1), h_grouped[unit_at(n + 1)[0]][:], "h")
+                    if layer_at(n + FRONT_AHEAD) == 0:
+                        transpose_h(unit_at(n + FRONT_AHEAD)[0])
+
+            if unit_at(n + FRONT_AHEAD) is not None:
+                for u in range(HALVES):
+                    noise(unit_at(n + FRONT_AHEAD), u)
+            if layer_at(n + 2) == 1:
+                chunk = unit_at(n + 2)[0]
+                quantise_moving(unit_at(n + 2), a_grouped[chunk][:].rearrange("p c t -> p (c t)"), "a")
+            if n == first_layer1 - 3:
+                mask_weights(1)
+            if n == first_layer1 - 2:
+                transpose_weights(1)
+            if n == first_layer1 - 1:
+                quantise_weights(1)

@@ -24,7 +24,6 @@ ROW_TILES = CHUNK // P
 BLOCKS = FEATURES // P
 HALVES = 2
 WORDS = FEATURES // 2
-FLOAT_MAX = 3.4028234663852886e38
 
 LAYER_LAG = 2
 LOAD_AHEAD = 6
@@ -237,13 +236,8 @@ def tile_scm_mlp_pa_t_kernel(tc, h_in, w, masks, mu, sigma, z, out):
 
         def regroup_a0(chunk):
             grouped = a_group_pool.tile([P, CHUNK, PACK], BF16, name="a_grouped", tag="a_grouped", align_bytes=64)
-            nc.gpsimd.tensor_scalar(
-                out=grouped[:],
-                in0=sums[(chunk, 0)][:].rearrange("q b c -> q c b"),
-                scalar1=FLOAT_MAX,
-                scalar2=0.0,
-                op0=ALU.min,
-                op1=ALU.max,
+            nc.vector.tensor_scalar_max(
+                out=grouped[:], in0=sums[(chunk, 0)][:].rearrange("q b c -> q c b"), scalar1=0.0
             )
             a_grouped[chunk] = grouped
 
@@ -259,10 +253,10 @@ def tile_scm_mlp_pa_t_kernel(tc, h_in, w, masks, mu, sigma, z, out):
                     nc.tensor.transpose(o_t[:, b, :], total[:, b, j * P : (j + 1) * P], ident_f32[:])
                 dst = rows[:, j, :].rearrange("p (u q e) -> p u q e", u=2, e=2)
                 src = o_t[:].rearrange("p (u e) q -> p u q e", e=2)
-                if j % 2 == 0:
-                    nc.scalar.activation(out=dst, in_=src, func=ACT.Relu)
-                else:
+                if j == 1 or (j == 3 and layer == 1):
                     nc.vector.tensor_scalar_max(out=dst, in0=src, scalar1=0.0)
+                else:
+                    nc.scalar.activation(out=dst, in_=src, func=ACT.Relu)
             dram = out[
                 chunk * CHUNK : (chunk + 1) * CHUNK, layer * FEATURES : (layer + 1) * FEATURES
             ].rearrange("(p j) f -> p j f", j=ROW_TILES)

@@ -24,8 +24,9 @@ ROW_TILES = CHUNK // P
 BLOCKS = FEATURES // P
 HALVES = 2
 WORDS = FEATURES // 2
+FLOAT_MAX = 3.4028234663852886e38
 
-LAYER_LAG = 2
+LAYER_LAG = 1
 LOAD_AHEAD = 6
 FRONT_AHEAD = 2
 
@@ -50,6 +51,10 @@ def tile_scm_mlp_pa_t_kernel(tc, h_in, w, masks, mu, sigma, z, out):
 
     def layer_at(i):
         return units[i][1] if 0 <= i < n_units else None
+
+    def next_layer0(i):
+        later = [m for m in range(i + 1, n_units) if units[m][1] == 0]
+        return later[0] if later else None
 
     with ExitStack() as ctx:
         const = ctx.enter_context(tc.tile_pool(name="const", bufs=1))
@@ -236,8 +241,13 @@ def tile_scm_mlp_pa_t_kernel(tc, h_in, w, masks, mu, sigma, z, out):
 
         def regroup_a0(chunk):
             grouped = a_group_pool.tile([P, CHUNK, PACK], BF16, name="a_grouped", tag="a_grouped", align_bytes=64)
-            nc.vector.tensor_scalar_max(
-                out=grouped[:], in0=sums[(chunk, 0)][:].rearrange("q b c -> q c b"), scalar1=0.0
+            nc.gpsimd.tensor_scalar(
+                out=grouped[:],
+                in0=sums[(chunk, 0)][:].rearrange("q b c -> q c b"),
+                scalar1=FLOAT_MAX,
+                scalar2=0.0,
+                op0=ALU.min,
+                op1=ALU.max,
             )
             a_grouped[chunk] = grouped
 
@@ -253,10 +263,10 @@ def tile_scm_mlp_pa_t_kernel(tc, h_in, w, masks, mu, sigma, z, out):
                     nc.tensor.transpose(o_t[:, b, :], total[:, b, j * P : (j + 1) * P], ident_f32[:])
                 dst = rows[:, j, :].rearrange("p (u q e) -> p u q e", u=2, e=2)
                 src = o_t[:].rearrange("p (u e) q -> p u q e", e=2)
-                if j == 1 or (j == 3 and layer == 1):
-                    nc.vector.tensor_scalar_max(out=dst, in0=src, scalar1=0.0)
-                else:
+                if j % 2 == 0:
                     nc.scalar.activation(out=dst, in_=src, func=ACT.Relu)
+                else:
+                    nc.vector.tensor_scalar_max(out=dst, in0=src, scalar1=0.0)
             dram = out[
                 chunk * CHUNK : (chunk + 1) * CHUNK, layer * FEATURES : (layer + 1) * FEATURES
             ].rearrange("(p j) f -> p j f", j=ROW_TILES)
@@ -264,23 +274,32 @@ def tile_scm_mlp_pa_t_kernel(tc, h_in, w, masks, mu, sigma, z, out):
                 out=dram[:, 2 * half : 2 * half + 2, :], in_=rows[:, 2 * half : 2 * half + 2, :]
             )
 
-        first_layer1 = units.index((0, 1))
+        def prepare_weights(layer):
+            mask_weights(layer)
+            transpose_weights(layer)
+            quantise_weights(layer)
+
+        def quantise_h(unit):
+            quantise_moving(unit, h_grouped[unit[0]][:], "h")
+
+        def quantise_a0(unit):
+            quantise_moving(unit, a_grouped[unit[0]][:].rearrange("p c t -> p (c t)"), "a")
 
         load_weights(0)
-        for i in range(LOAD_AHEAD):
-            if i == first_layer1:
-                load_weights(1)
+        load_unit(units[0])
+        load_weights(1)
+        for i in range(1, LOAD_AHEAD):
             load_unit(units[i])
 
-        mask_weights(0)
-        transpose_weights(0)
-        quantise_weights(0)
-        for i in range(FRONT_AHEAD):
-            transpose_h(units[i][0])
-            if i == 0:
-                quantise_moving(units[i], h_grouped[units[i][0]][:], "h")
-            for u in range(HALVES):
-                noise(units[i], u)
+        prepare_weights(0)
+        transpose_h(units[0][0])
+        quantise_h(units[0])
+        for u in range(HALVES):
+            noise(units[0], u)
+        prepare_weights(1)
+        transpose_h(units[next_layer0(0)][0])
+        for u in range(HALVES):
+            noise(units[1], u)
 
         for n in range(n_units + 1):
             if unit_at(n + LOAD_AHEAD) is not None:
@@ -294,20 +313,13 @@ def tile_scm_mlp_pa_t_kernel(tc, h_in, w, masks, mu, sigma, z, out):
                 if unit_at(n - 1) is not None:
                     finish(unit_at(n - 1), half)
                 if half == 0:
-                    if layer_at(n + 1) == 0:
-                        quantise_moving(unit_at(n + 1), h_grouped[unit_at(n + 1)[0]][:], "h")
-                    if layer_at(n + FRONT_AHEAD) == 0:
-                        transpose_h(unit_at(n + FRONT_AHEAD)[0])
+                    if layer_at(n) == 0 and next_layer0(n) is not None:
+                        quantise_h(units[next_layer0(n)])
+                    if layer_at(n + 1) == 1:
+                        quantise_a0(unit_at(n + 1))
+                    if layer_at(n + 1) == 0 and next_layer0(n + 1) is not None:
+                        transpose_h(units[next_layer0(n + 1)][0])
 
             if unit_at(n + FRONT_AHEAD) is not None:
                 for u in range(HALVES):
                     noise(unit_at(n + FRONT_AHEAD), u)
-            if layer_at(n + 2) == 1:
-                chunk = unit_at(n + 2)[0]
-                quantise_moving(unit_at(n + 2), a_grouped[chunk][:].rearrange("p c t -> p (c t)"), "a")
-            if n == first_layer1 - 3:
-                mask_weights(1)
-            if n == first_layer1 - 2:
-                transpose_weights(1)
-            if n == first_layer1 - 1:
-                quantise_weights(1)

@@ -263,10 +263,10 @@ def tile_scm_mlp_pa_t_kernel(tc, h_in, w, masks, mu, sigma, z, out):
                     nc.tensor.transpose(o_t[:, b, :], total[:, b, j * P : (j + 1) * P], ident_f32[:])
                 dst = rows[:, j, :].rearrange("p (u q e) -> p u q e", u=2, e=2)
                 src = o_t[:].rearrange("p (u e) q -> p u q e", e=2)
-                if j % 2 == 0:
-                    nc.scalar.activation(out=dst, in_=src, func=ACT.Relu)
-                else:
+                if (layer == 1 and j == 3) or (layer == 0 and j != 2):
                     nc.vector.tensor_scalar_max(out=dst, in0=src, scalar1=0.0)
+                else:
+                    nc.scalar.activation(out=dst, in_=src, func=ACT.Relu)
             dram = out[
                 chunk * CHUNK : (chunk + 1) * CHUNK, layer * FEATURES : (layer + 1) * FEATURES
             ].rearrange("(p j) f -> p j f", j=ROW_TILES)

@@ -14,8 +14,11 @@ ACT = mybir.ActivationFunctionType
 ALU = mybir.AluOpType
 
 P = 128
-PACK = 4
+PAIR = 2
+SIDES = 2
+PACK = SIDES * PAIR
 FEATURES = P * PACK
+WORDS = FEATURES // PAIR
 LAYERS = 2
 ROWS = 4096
 CHUNK = 512
@@ -23,12 +26,21 @@ CHUNKS = ROWS // CHUNK
 ROW_TILES = CHUNK // P
 BLOCKS = FEATURES // P
 HALVES = 2
-WORDS = FEATURES // 2
+PER_HALF = BLOCKS // HALVES
 FLOAT_MAX = 3.4028234663852886e38
 
 LAYER_LAG = 1
 LOAD_AHEAD = 6
-FRONT_AHEAD = 2
+NOISE_AHEAD = 2
+
+MX_BANKS = 3
+TRANSPOSE_BANKS = 5
+H_LOADS = 4
+SUM_TILES = 7
+H_GROUPED = 2
+A_GROUPED = 3
+CODE_TILES = 3
+OUT_TILES = 4
 
 
 def unit_order():
@@ -59,15 +71,15 @@ def tile_scm_mlp_pa_t_kernel(tc, h_in, w, masks, mu, sigma, z, out):
     with ExitStack() as ctx:
         const = ctx.enter_context(tc.tile_pool(name="const", bufs=1))
         weights = ctx.enter_context(tc.tile_pool(name="weights", bufs=1))
-        h_pool = ctx.enter_context(tc.tile_pool(name="h_pool", bufs=4))
+        h_pool = ctx.enter_context(tc.tile_pool(name="h_pool", bufs=H_LOADS))
         z_pool = ctx.enter_context(tc.tile_pool(name="z_pool", bufs=LOAD_AHEAD))
-        sum_pool = ctx.enter_context(tc.tile_pool(name="sum_pool", bufs=7))
-        h_group_pool = ctx.enter_context(tc.tile_pool(name="h_group_pool", bufs=2))
-        a_group_pool = ctx.enter_context(tc.tile_pool(name="a_group_pool", bufs=3))
-        code_pool = ctx.enter_context(tc.tile_pool(name="code_pool", bufs=3))
-        out_pool = ctx.enter_context(tc.tile_pool(name="out_pool", bufs=4))
-        psum_pre = ctx.enter_context(tc.psum_pool(name="psum_pre", bufs=3))
-        psum_tr = ctx.enter_context(tc.psum_pool(name="psum_tr", bufs=5))
+        sum_pool = ctx.enter_context(tc.tile_pool(name="sum_pool", bufs=SUM_TILES))
+        h_group_pool = ctx.enter_context(tc.tile_pool(name="h_group_pool", bufs=H_GROUPED))
+        a_group_pool = ctx.enter_context(tc.tile_pool(name="a_group_pool", bufs=A_GROUPED))
+        code_pool = ctx.enter_context(tc.tile_pool(name="code_pool", bufs=CODE_TILES))
+        out_pool = ctx.enter_context(tc.tile_pool(name="out_pool", bufs=OUT_TILES))
+        psum_pre = ctx.enter_context(tc.psum_pool(name="psum_pre", bufs=MX_BANKS))
+        psum_tr = ctx.enter_context(tc.psum_pool(name="psum_tr", bufs=TRANSPOSE_BANKS))
         ctx.enter_context(tc.manual_schedule())
 
         h_sb = {}
@@ -104,12 +116,12 @@ def tile_scm_mlp_pa_t_kernel(tc, h_in, w, masks, mu, sigma, z, out):
         def load_weights(layer):
             w_sb[layer] = weights.tile([P, BLOCKS, FEATURES], BF16, name="w_raw%d" % layer)
             m_sb[layer] = weights.tile([P, BLOCKS, FEATURES], BF16, name="m_raw%d" % layer)
-            for half in range(HALVES):
+            for u in range(SIDES):
                 for src, raw in ((w, w_sb[layer]), (masks, m_sb[layer])):
                     nc.sync.dma_start(
-                        out=raw[:, 2 * half : 2 * half + 2, :].rearrange("q e k -> q (e k)"),
-                        in_=src[layer][2 * half * P : (2 * half + 2) * P, :].rearrange(
-                            "(q e) k -> q (e k)", e=2
+                        out=raw[:, PAIR * u : PAIR * (u + 1), :].rearrange("q e k -> q (e k)"),
+                        in_=src[layer][PAIR * u * P : PAIR * (u + 1) * P, :].rearrange(
+                            "(q e) k -> q (e k)", e=PAIR
                         ),
                     )
 
@@ -125,14 +137,14 @@ def tile_scm_mlp_pa_t_kernel(tc, h_in, w, masks, mu, sigma, z, out):
                 for src, dst, name in ((sigma, noise_scale, "sg%d"), (mu, noise_bias, "mu%d")):
                     raw = const.tile([P, BLOCKS], BF16, name=name % layer)
                     nc.scalar.dma_start(
-                        out=raw[:].rearrange("q (u e) -> q u e", e=2),
-                        in_=src[layer].rearrange("(u q e) -> q u e", u=2, e=2),
+                        out=raw[:].rearrange("q (u e) -> q u e", e=PAIR),
+                        in_=src[layer].rearrange("(u q e) -> q u e", u=SIDES, e=PAIR),
                     )
                     nc.vector.tensor_copy(out=dst[:, layer, :], in_=raw[:])
 
         def mask_weights(layer):
-            for half in range(HALVES):
-                blocks = slice(2 * half, 2 * half + 2)
+            for u in range(SIDES):
+                blocks = slice(PAIR * u, PAIR * (u + 1))
                 nc.vector.tensor_tensor(
                     out=w_sb[layer][:, blocks, :],
                     in0=w_sb[layer][:, blocks, :],
@@ -143,15 +155,15 @@ def tile_scm_mlp_pa_t_kernel(tc, h_in, w, masks, mu, sigma, z, out):
         def transpose_weights(layer):
             grouped = weights.tile([P, FEATURES, PACK], BF16, name="w_grouped%d" % layer, align_bytes=64)
             for half in range(HALVES):
-                w_t = psum_tr.tile([P, 2, PACK, P], BF16, name="w_t", tag="tr")
-                for bb in range(2):
-                    k_view = w_sb[layer][:, 2 * half + bb, :].rearrange(
-                        "q (u p e) -> q u e p", u=2, e=2
+                w_t = psum_tr.tile([P, PER_HALF, PACK, P], BF16, name="w_t", tag="tr")
+                for bb in range(PER_HALF):
+                    k_view = w_sb[layer][:, PER_HALF * half + bb, :].rearrange(
+                        "q (u p e) -> q u e p", u=SIDES, e=PAIR
                     )
                     for t in range(PACK):
-                        nc.tensor.transpose(w_t[:, bb, t, :], k_view[:, t // 2, t % 2, :], ident_bf16[:])
-                dst = grouped[:, 2 * half * P : (2 * half + 2) * P, :].rearrange(
-                    "p (bb q) t -> p bb q t", bb=2
+                        nc.tensor.transpose(w_t[:, bb, t, :], k_view[:, t // PAIR, t % PAIR, :], ident_bf16[:])
+                dst = grouped[:, PER_HALF * half * P : PER_HALF * (half + 1) * P, :].rearrange(
+                    "p (bb q) t -> p bb q t", bb=PER_HALF
                 )
                 if half == 0:
                     nc.scalar.copy(out=dst, in_=w_t[:].rearrange("p bb t q -> p bb q t"))
@@ -163,7 +175,7 @@ def tile_scm_mlp_pa_t_kernel(tc, h_in, w, masks, mu, sigma, z, out):
             w_codes[layer] = weights.tile([P, FEATURES], U32, name="w_codes%d" % layer, align_bytes=64)
             w_scales[layer] = weights.tile([P, FEATURES], U8, name="w_scales%d" % layer, align_bytes=64)
             for half in range(HALVES):
-                cols = slice(2 * half * P, (2 * half + 2) * P)
+                cols = slice(PER_HALF * half * P, PER_HALF * (half + 1) * P)
                 nc.vector.quantize_mx(
                     out=w_codes[layer][:, cols].bitcast(FP8X4),
                     scales=w_scales[layer][:, cols],
@@ -173,19 +185,19 @@ def tile_scm_mlp_pa_t_kernel(tc, h_in, w, masks, mu, sigma, z, out):
         def transpose_h(chunk):
             words = h_sb[chunk][:].bitcast(F32)
             grouped = h_group_pool.tile([P, CHUNK * PACK], BF16, name="h_grouped", tag="h_grouped", align_bytes=64)
-            grouped_words = grouped[:].bitcast(F32).rearrange("p (c u) -> p c u", u=2)
+            grouped_words = grouped[:].bitcast(F32).rearrange("p (c u) -> p c u", u=SIDES)
             for half in range(HALVES):
-                h_t = psum_tr.tile([P, 2, 2 * P], F32, name="h_t", tag="tr")
-                for jj in range(2):
-                    j = 2 * half + jj
-                    for u in range(2):
+                h_t = psum_tr.tile([P, SIDES, PER_HALF * P], F32, name="h_t", tag="tr")
+                for jj in range(PER_HALF):
+                    j = PER_HALF * half + jj
+                    for u in range(SIDES):
                         nc.tensor.transpose(
                             h_t[:, u, jj * P : (jj + 1) * P],
                             words[:, j * WORDS + u * P : j * WORDS + (u + 1) * P],
                             ident_f32[:],
                         )
                 nc.scalar.copy(
-                    out=grouped_words[:, 2 * half * P : (2 * half + 2) * P, :],
+                    out=grouped_words[:, PER_HALF * half * P : PER_HALF * (half + 1) * P, :],
                     in_=h_t[:].rearrange("p u c -> p c u"),
                 )
             h_grouped[chunk] = grouped
@@ -197,8 +209,14 @@ def tile_scm_mlp_pa_t_kernel(tc, h_in, w, masks, mu, sigma, z, out):
                 out=x_codes[unit][:].bitcast(FP8X4), scales=x_scales[unit][:], in_=grouped_flat
             )
 
+        def quantise_h(unit):
+            quantise_moving(unit, h_grouped[unit[0]][:], "h")
+
+        def quantise_a0(unit):
+            quantise_moving(unit, a_grouped[unit[0]][:].rearrange("p c t -> p (c t)"), "a")
+
         def noise(unit, u):
-            chunk, layer = unit
+            layer = unit[1]
             words = z_sb[unit][:].bitcast(F32)
             if u == 0:
                 sums[unit] = sum_pool.tile([P, BLOCKS, CHUNK], F32, name="total", tag="total")
@@ -210,9 +228,9 @@ def tile_scm_mlp_pa_t_kernel(tc, h_in, w, masks, mu, sigma, z, out):
                     words[:, j * WORDS + u * P : j * WORDS + (u + 1) * P],
                     ident_f32[:],
                 )
-            pairs = z_t[:].bitcast(BF16).rearrange("q (c e) -> q c e", e=2)
-            for e in range(2):
-                b = 2 * u + e
+            pairs = z_t[:].bitcast(BF16).rearrange("q (c e) -> q c e", e=PAIR)
+            for e in range(PAIR):
+                b = PAIR * u + e
                 nc.scalar.activation(
                     out=total[:, b, :],
                     in_=pairs[:, :, e],
@@ -222,9 +240,9 @@ def tile_scm_mlp_pa_t_kernel(tc, h_in, w, masks, mu, sigma, z, out):
                 )
 
         def multiply_and_add(unit, half):
-            chunk, layer = unit
+            layer = unit[1]
             total = sums[unit]
-            for b in range(2 * half, 2 * half + 2):
+            for b in range(PER_HALF * half, PER_HALF * (half + 1)):
                 acc = psum_pre.tile([P, CHUNK], F32, name="acc", tag="acc")
                 nc.tensor.matmul_mx(
                     out=acc[:],
@@ -236,7 +254,7 @@ def tile_scm_mlp_pa_t_kernel(tc, h_in, w, masks, mu, sigma, z, out):
                     stop=True,
                 )
                 accs[b] = acc
-            for b in range(2 * half, 2 * half + 2):
+            for b in range(PER_HALF * half, PER_HALF * (half + 1)):
                 nc.vector.tensor_tensor(out=total[:, b, :], in0=accs[b][:], in1=total[:, b, :], op=ALU.add)
 
         def regroup_a0(chunk):
@@ -251,39 +269,33 @@ def tile_scm_mlp_pa_t_kernel(tc, h_in, w, masks, mu, sigma, z, out):
             )
             a_grouped[chunk] = grouped
 
-        def finish(unit, half):
+        def finish(unit, half, scalar_copies_h):
             chunk, layer = unit
             total = sums[unit]
             if half == 0:
                 out_sb[unit] = out_pool.tile([P, ROW_TILES, FEATURES], F32, name="out_rows", tag="out_rows")
             rows = out_sb[unit]
-            for j in range(2 * half, 2 * half + 2):
+            tiles = slice(PER_HALF * half, PER_HALF * (half + 1))
+            for j in range(PER_HALF * half, PER_HALF * (half + 1)):
                 o_t = psum_tr.tile([P, BLOCKS, P], F32, name="o_t", tag="tr")
                 for b in range(BLOCKS):
                     nc.tensor.transpose(o_t[:, b, :], total[:, b, j * P : (j + 1) * P], ident_f32[:])
-                dst = rows[:, j, :].rearrange("p (u q e) -> p u q e", u=2, e=2)
-                src = o_t[:].rearrange("p (u e) q -> p u q e", e=2)
-                if (layer == 1 and j == 3) or (layer == 0 and j != 2):
+                dst = rows[:, j, :].rearrange("p (u q e) -> p u q e", u=SIDES, e=PAIR)
+                src = o_t[:].rearrange("p (u e) q -> p u q e", e=PAIR)
+                on_vector = (j != ROW_TILES - 2) if scalar_copies_h else (j == ROW_TILES - 1)
+                if on_vector:
                     nc.vector.tensor_scalar_max(out=dst, in0=src, scalar1=0.0)
                 else:
                     nc.scalar.activation(out=dst, in_=src, func=ACT.Relu)
             dram = out[
                 chunk * CHUNK : (chunk + 1) * CHUNK, layer * FEATURES : (layer + 1) * FEATURES
             ].rearrange("(p j) f -> p j f", j=ROW_TILES)
-            nc.sync.dma_start(
-                out=dram[:, 2 * half : 2 * half + 2, :], in_=rows[:, 2 * half : 2 * half + 2, :]
-            )
+            nc.sync.dma_start(out=dram[:, tiles, :], in_=rows[:, tiles, :])
 
         def prepare_weights(layer):
             mask_weights(layer)
             transpose_weights(layer)
             quantise_weights(layer)
-
-        def quantise_h(unit):
-            quantise_moving(unit, h_grouped[unit[0]][:], "h")
-
-        def quantise_a0(unit):
-            quantise_moving(unit, a_grouped[unit[0]][:].rearrange("p c t -> p (c t)"), "a")
 
         load_weights(0)
         load_unit(units[0])
@@ -294,16 +306,17 @@ def tile_scm_mlp_pa_t_kernel(tc, h_in, w, masks, mu, sigma, z, out):
         prepare_weights(0)
         transpose_h(units[0][0])
         quantise_h(units[0])
-        for u in range(HALVES):
+        for u in range(SIDES):
             noise(units[0], u)
         prepare_weights(1)
         transpose_h(units[next_layer0(0)][0])
-        for u in range(HALVES):
+        for u in range(SIDES):
             noise(units[1], u)
 
         for n in range(n_units + 1):
             if unit_at(n + LOAD_AHEAD) is not None:
                 load_unit(unit_at(n + LOAD_AHEAD))
+            h_next = next_layer0(n + 1) if layer_at(n + 1) == 0 else None
 
             for half in range(HALVES):
                 if unit_at(n) is not None:
@@ -311,15 +324,15 @@ def tile_scm_mlp_pa_t_kernel(tc, h_in, w, masks, mu, sigma, z, out):
                     if half == HALVES - 1 and layer_at(n) == 0:
                         regroup_a0(unit_at(n)[0])
                 if unit_at(n - 1) is not None:
-                    finish(unit_at(n - 1), half)
+                    finish(unit_at(n - 1), half, h_next is not None)
                 if half == 0:
                     if layer_at(n) == 0 and next_layer0(n) is not None:
                         quantise_h(units[next_layer0(n)])
                     if layer_at(n + 1) == 1:
                         quantise_a0(unit_at(n + 1))
-                    if layer_at(n + 1) == 0 and next_layer0(n + 1) is not None:
-                        transpose_h(units[next_layer0(n + 1)][0])
+                    if h_next is not None:
+                        transpose_h(units[h_next][0])
 
-            if unit_at(n + FRONT_AHEAD) is not None:
-                for u in range(HALVES):
-                    noise(unit_at(n + FRONT_AHEAD), u)
+            if unit_at(n + NOISE_AHEAD) is not None:
+                for u in range(SIDES):
+                    noise(unit_at(n + NOISE_AHEAD), u)

@@ -33,6 +33,8 @@ LAYER_LAG = 1
 LOAD_AHEAD = 6
 NOISE_AHEAD = 2
 
+JOINED = range(1, 6)
+
 MX_BANKS = 3
 TRANSPOSE_BANKS = 5
 H_LOADS = 4
@@ -107,23 +109,28 @@ def tile_scm_mlp_pa_t_kernel(tc, h_in, w, masks, mu, sigma, z, out):
             )
             return rows
 
-        def load_unit(unit):
-            chunk, layer = unit
-            if layer == 0:
-                h_sb[chunk] = load_rows(h_pool, h_in, chunk, "h_rows")
-            z_sb[unit] = load_rows(z_pool, z[layer], chunk, "z_rows")
+        def load_h(chunk):
+            h_sb[chunk] = load_rows(h_pool, h_in, chunk, "h_rows")
 
-        def load_weights(layer):
-            w_sb[layer] = weights.tile([P, BLOCKS, FEATURES], BF16, name="w_raw%d" % layer)
-            m_sb[layer] = weights.tile([P, BLOCKS, FEATURES], BF16, name="m_raw%d" % layer)
-            for u in range(SIDES):
-                for src, raw in ((w, w_sb[layer]), (masks, m_sb[layer])):
-                    nc.sync.dma_start(
-                        out=raw[:, PAIR * u : PAIR * (u + 1), :].rearrange("q e k -> q (e k)"),
-                        in_=src[layer][PAIR * u * P : PAIR * (u + 1) * P, :].rearrange(
-                            "(q e) k -> q (e k)", e=PAIR
-                        ),
-                    )
+        def load_z(unit):
+            z_sb[unit] = load_rows(z_pool, z[unit[1]], unit[0], "z_rows")
+
+        def load_unit(unit):
+            if unit[1] == 0:
+                load_h(unit[0])
+            load_z(unit)
+
+        def load_weights(layer, u):
+            if u == 0:
+                w_sb[layer] = weights.tile([P, BLOCKS, FEATURES], BF16, name="w_raw%d" % layer)
+                m_sb[layer] = weights.tile([P, BLOCKS, FEATURES], BF16, name="m_raw%d" % layer)
+            for src, raw in ((w, w_sb[layer]), (masks, m_sb[layer])):
+                nc.sync.dma_start(
+                    out=raw[:, PAIR * u : PAIR * (u + 1), :].rearrange("q e k -> q (e k)"),
+                    in_=src[layer][PAIR * u * P : PAIR * (u + 1) * P, :].rearrange(
+                        "(q e) k -> q (e k)", e=PAIR
+                    ),
+                )
 
         ident_f32 = const.tile([P, P], F32)
         make_identity(nc, ident_f32[:])
@@ -141,46 +148,48 @@ def tile_scm_mlp_pa_t_kernel(tc, h_in, w, masks, mu, sigma, z, out):
                         in_=src[layer].rearrange("(u q e) -> q u e", u=SIDES, e=PAIR),
                     )
                     nc.vector.tensor_copy(out=dst[:, layer, :], in_=raw[:])
+        warm = const.tile([P, 1], F32)
+        nc.scalar.activation(out=warm[:], in_=ident_f32[:, 0:1], func=ACT.Exp)
 
-        def mask_weights(layer):
-            for u in range(SIDES):
-                blocks = slice(PAIR * u, PAIR * (u + 1))
-                nc.vector.tensor_tensor(
-                    out=w_sb[layer][:, blocks, :],
-                    in0=w_sb[layer][:, blocks, :],
-                    in1=m_sb[layer][:, blocks, :],
-                    op=ALU.mult,
-                )
+        def mask_weights(layer, u):
+            blocks = slice(PAIR * u, PAIR * (u + 1))
+            nc.vector.tensor_tensor(
+                out=w_sb[layer][:, blocks, :],
+                in0=w_sb[layer][:, blocks, :],
+                in1=m_sb[layer][:, blocks, :],
+                op=ALU.mult,
+            )
 
-        def transpose_weights(layer):
-            grouped = weights.tile([P, FEATURES, PACK], BF16, name="w_grouped%d" % layer, align_bytes=64)
-            for half in range(HALVES):
-                w_t = psum_tr.tile([P, PER_HALF, PACK, P], BF16, name="w_t", tag="tr")
-                for bb in range(PER_HALF):
-                    k_view = w_sb[layer][:, PER_HALF * half + bb, :].rearrange(
-                        "q (u p e) -> q u e p", u=SIDES, e=PAIR
-                    )
-                    for t in range(PACK):
-                        nc.tensor.transpose(w_t[:, bb, t, :], k_view[:, t // PAIR, t % PAIR, :], ident_bf16[:])
-                dst = grouped[:, PER_HALF * half * P : PER_HALF * (half + 1) * P, :].rearrange(
-                    "p (bb q) t -> p bb q t", bb=PER_HALF
+        def transpose_weights(layer, half, engine):
+            if half == 0:
+                w_grouped[layer] = weights.tile(
+                    [P, FEATURES, PACK], BF16, name="w_grouped%d" % layer, align_bytes=64
                 )
-                if half == 0:
-                    nc.scalar.copy(out=dst, in_=w_t[:].rearrange("p bb t q -> p bb q t"))
-                else:
-                    nc.vector.tensor_copy(out=dst, in_=w_t[:].rearrange("p bb t q -> p bb q t"))
-            w_grouped[layer] = grouped
+            w_t = psum_tr.tile([P, PER_HALF, PACK, P], BF16, name="w_t", tag="tr")
+            for bb in range(PER_HALF):
+                k_view = w_sb[layer][:, PER_HALF * half + bb, :].rearrange(
+                    "q (u p e) -> q u e p", u=SIDES, e=PAIR
+                )
+                for t in range(PACK):
+                    nc.tensor.transpose(w_t[:, bb, t, :], k_view[:, t // PAIR, t % PAIR, :], ident_bf16[:])
+            dst = w_grouped[layer][:, PER_HALF * half * P : PER_HALF * (half + 1) * P, :].rearrange(
+                "p (bb q) t -> p bb q t", bb=PER_HALF
+            )
+            if engine == "scalar":
+                nc.scalar.copy(out=dst, in_=w_t[:].rearrange("p bb t q -> p bb q t"))
+            else:
+                nc.vector.tensor_copy(out=dst, in_=w_t[:].rearrange("p bb t q -> p bb q t"))
 
-        def quantise_weights(layer):
-            w_codes[layer] = weights.tile([P, FEATURES], U32, name="w_codes%d" % layer, align_bytes=64)
-            w_scales[layer] = weights.tile([P, FEATURES], U8, name="w_scales%d" % layer, align_bytes=64)
-            for half in range(HALVES):
-                cols = slice(PER_HALF * half * P, PER_HALF * (half + 1) * P)
-                nc.vector.quantize_mx(
-                    out=w_codes[layer][:, cols].bitcast(FP8X4),
-                    scales=w_scales[layer][:, cols],
-                    in_=w_grouped[layer][:, cols, :].rearrange("p c t -> p (c t)"),
-                )
+        def quantise_weights(layer, half):
+            if half == 0:
+                w_codes[layer] = weights.tile([P, FEATURES], U32, name="w_codes%d" % layer, align_bytes=64)
+                w_scales[layer] = weights.tile([P, FEATURES], U8, name="w_scales%d" % layer, align_bytes=64)
+            cols = slice(PER_HALF * half * P, PER_HALF * (half + 1) * P)
+            nc.vector.quantize_mx(
+                out=w_codes[layer][:, cols].bitcast(FP8X4),
+                scales=w_scales[layer][:, cols],
+                in_=w_grouped[layer][:, cols, :].rearrange("p c t -> p (c t)"),
+            )
 
         def transpose_h(chunk):
             words = h_sb[chunk][:].bitcast(F32)
@@ -269,54 +278,67 @@ def tile_scm_mlp_pa_t_kernel(tc, h_in, w, masks, mu, sigma, z, out):
             )
             a_grouped[chunk] = grouped
 
-        def finish(unit, half, scalar_copies_h):
+        def finish(unit, half, on_vector):
             chunk, layer = unit
             total = sums[unit]
-            if half == 0:
-                out_sb[unit] = out_pool.tile([P, ROW_TILES, FEATURES], F32, name="out_rows", tag="out_rows")
-            rows = out_sb[unit]
+            if half == 0 and layer == 0:
+                out_sb[chunk] = out_pool.tile([P, ROW_TILES, LAYERS * FEATURES], F32, name="out_rows", tag="out_rows")
+            rows = out_sb[chunk]
+            features = slice(layer * FEATURES, (layer + 1) * FEATURES)
             tiles = slice(PER_HALF * half, PER_HALF * (half + 1))
             for j in range(PER_HALF * half, PER_HALF * (half + 1)):
                 o_t = psum_tr.tile([P, BLOCKS, P], F32, name="o_t", tag="tr")
                 for b in range(BLOCKS):
                     nc.tensor.transpose(o_t[:, b, :], total[:, b, j * P : (j + 1) * P], ident_f32[:])
-                dst = rows[:, j, :].rearrange("p (u q e) -> p u q e", u=SIDES, e=PAIR)
+                dst = rows[:, j, features].rearrange("p (u q e) -> p u q e", u=SIDES, e=PAIR)
                 src = o_t[:].rearrange("p (u e) q -> p u q e", e=PAIR)
-                on_vector = (j != ROW_TILES - 2) if scalar_copies_h else (j == ROW_TILES - 1)
-                if on_vector:
+                if j in on_vector:
                     nc.vector.tensor_scalar_max(out=dst, in0=src, scalar1=0.0)
                 else:
                     nc.scalar.activation(out=dst, in_=src, func=ACT.Relu)
-            dram = out[
-                chunk * CHUNK : (chunk + 1) * CHUNK, layer * FEATURES : (layer + 1) * FEATURES
-            ].rearrange("(p j) f -> p j f", j=ROW_TILES)
-            nc.sync.dma_start(out=dram[:, tiles, :], in_=rows[:, tiles, :])
+            dram = out[chunk * CHUNK : (chunk + 1) * CHUNK, :].rearrange("(p j) f -> p j f", j=ROW_TILES)
+            if chunk not in JOINED:
+                nc.sync.dma_start(out=dram[:, tiles, features], in_=rows[:, tiles, features])
+            elif layer == LAYERS - 1:
+                nc.sync.dma_start(out=dram[:, tiles, :], in_=rows[:, tiles, :])
 
-        def prepare_weights(layer):
-            mask_weights(layer)
-            transpose_weights(layer)
-            quantise_weights(layer)
-
-        load_weights(0)
-        load_unit(units[0])
-        load_weights(1)
-        for i in range(1, LOAD_AHEAD):
+        load_z(units[0])
+        load_weights(0, 0)
+        load_h(units[0][0])
+        load_weights(0, 1)
+        load_z(units[1])
+        load_h(units[1][0])
+        load_weights(1, 0)
+        load_weights(1, 1)
+        for i in range(2, LOAD_AHEAD):
             load_unit(units[i])
 
-        prepare_weights(0)
-        transpose_h(units[0][0])
-        quantise_h(units[0])
         for u in range(SIDES):
             noise(units[0], u)
-        prepare_weights(1)
-        transpose_h(units[next_layer0(0)][0])
+        transpose_h(units[0][0])
+        for half in range(HALVES):
+            mask_weights(0, half)
+        for half in range(HALVES):
+            transpose_weights(0, half, "vector")
+        for half in range(HALVES):
+            quantise_weights(0, half)
+        quantise_h(units[0])
         for u in range(SIDES):
             noise(units[1], u)
+        transpose_h(units[1][0])
+
+        def relu_copies_on_vector(n, copies_h):
+            if n == n_units:
+                return (1, 3)
+            if unit_at(n + NOISE_AHEAD) is None:
+                return ()
+            return (0, 1, 3) if copies_h else (3,)
 
         for n in range(n_units + 1):
             if unit_at(n + LOAD_AHEAD) is not None:
                 load_unit(unit_at(n + LOAD_AHEAD))
             h_next = next_layer0(n + 1) if layer_at(n + 1) == 0 else None
+            on_vector = relu_copies_on_vector(n, h_next is not None)
 
             for half in range(HALVES):
                 if unit_at(n) is not None:
@@ -324,14 +346,24 @@ def tile_scm_mlp_pa_t_kernel(tc, h_in, w, masks, mu, sigma, z, out):
                     if half == HALVES - 1 and layer_at(n) == 0:
                         regroup_a0(unit_at(n)[0])
                 if unit_at(n - 1) is not None:
-                    finish(unit_at(n - 1), half, h_next is not None)
+                    finish(unit_at(n - 1), half, on_vector)
                 if half == 0:
                     if layer_at(n) == 0 and next_layer0(n) is not None:
                         quantise_h(units[next_layer0(n)])
+                    if n == 0:
+                        for u in range(SIDES):
+                            mask_weights(1, u)
+                    if n == 1:
+                        for u in range(HALVES):
+                            quantise_weights(1, u)
                     if layer_at(n + 1) == 1:
                         quantise_a0(unit_at(n + 1))
-                    if h_next is not None:
+                    if h_next is not None and n > 0:
                         transpose_h(units[h_next][0])
+                if n == 0 and half == HALVES - 1:
+                    for u in range(HALVES):
+                        transpose_weights(1, u, "scalar")
+                    transpose_h(units[h_next][0])
 
             if unit_at(n + NOISE_AHEAD) is not None:
                 for u in range(SIDES):

@@ -33,7 +33,7 @@ LAYER_LAG = 1
 LOAD_AHEAD = 6
 NOISE_AHEAD = 2
 
-JOINED = range(1, 6)
+JOINED = range(1, 5)
 
 MX_BANKS = 3
 TRANSPOSE_BANKS = 5
@@ -297,7 +297,10 @@ def tile_scm_mlp_pa_t_kernel(tc, h_in, w, masks, mu, sigma, z, out):
                 else:
                     nc.scalar.activation(out=dst, in_=src, func=ACT.Relu)
             dram = out[chunk * CHUNK : (chunk + 1) * CHUNK, :].rearrange("(p j) f -> p j f", j=ROW_TILES)
-            if chunk not in JOINED:
+            if unit == units[-1]:
+                for j in range(PER_HALF * half, PER_HALF * (half + 1)):
+                    nc.sync.dma_start(out=dram[:, j, features], in_=rows[:, j, features])
+            elif chunk not in JOINED:
                 nc.sync.dma_start(out=dram[:, tiles, features], in_=rows[:, tiles, features])
             elif layer == LAYERS - 1:
                 nc.sync.dma_start(out=dram[:, tiles, :], in_=rows[:, tiles, :])
@@ -345,6 +348,8 @@ def tile_scm_mlp_pa_t_kernel(tc, h_in, w, masks, mu, sigma, z, out):
                     multiply_and_add(unit_at(n), half)
                     if half == HALVES - 1 and layer_at(n) == 0:
                         regroup_a0(unit_at(n)[0])
+                if unit_at(n + NOISE_AHEAD) is not None:
+                    noise(unit_at(n + NOISE_AHEAD), half)
                 if unit_at(n - 1) is not None:
                     finish(unit_at(n - 1), half, on_vector)
                 if half == 0:
@@ -364,7 +369,3 @@ def tile_scm_mlp_pa_t_kernel(tc, h_in, w, masks, mu, sigma, z, out):
                     for u in range(HALVES):
                         transpose_weights(1, u, "scalar")
                     transpose_h(units[h_next][0])
-
-            if unit_at(n + NOISE_AHEAD) is not None:
-                for u in range(SIDES):
-                    noise(unit_at(n + NOISE_AHEAD), u)

@@ -23,6 +23,8 @@ LAYERS = 2
 ROWS = 4096
 CHUNK = 512
 CHUNKS = ROWS // CHUNK
+GROUP = 2
+GROUPS = CHUNKS // GROUP
 ROW_TILES = CHUNK // P
 BLOCKS = FEATURES // P
 HALVES = 2
@@ -30,15 +32,14 @@ PER_HALF = BLOCKS // HALVES
 FLOAT_MAX = 3.4028234663852886e38
 
 LAYER_LAG = 1
-LOAD_AHEAD = 6
+LOAD_GROUPS = 2
 NOISE_AHEAD = 2
 
-JOINED = range(1, 5)
+JOINED = range(0, 5)
 
 MX_BANKS = 3
 TRANSPOSE_BANKS = 5
-H_LOADS = 4
-SUM_TILES = 7
+SUM_TILES = 6
 H_GROUPED = 2
 A_GROUPED = 3
 CODE_TILES = 3
@@ -73,8 +74,8 @@ def tile_scm_mlp_pa_t_kernel(tc, h_in, w, masks, mu, sigma, z, out):
     with ExitStack() as ctx:
         const = ctx.enter_context(tc.tile_pool(name="const", bufs=1))
         weights = ctx.enter_context(tc.tile_pool(name="weights", bufs=1))
-        h_pool = ctx.enter_context(tc.tile_pool(name="h_pool", bufs=H_LOADS))
-        z_pool = ctx.enter_context(tc.tile_pool(name="z_pool", bufs=LOAD_AHEAD))
+        h_pool = ctx.enter_context(tc.tile_pool(name="h_pool", bufs=LOAD_GROUPS))
+        z_pool = ctx.enter_context(tc.tile_pool(name="z_pool", bufs=LOAD_GROUPS))
         sum_pool = ctx.enter_context(tc.tile_pool(name="sum_pool", bufs=SUM_TILES))
         h_group_pool = ctx.enter_context(tc.tile_pool(name="h_group_pool", bufs=H_GROUPED))
         a_group_pool = ctx.enter_context(tc.tile_pool(name="a_group_pool", bufs=A_GROUPED))
@@ -99,26 +100,42 @@ def tile_scm_mlp_pa_t_kernel(tc, h_in, w, masks, mu, sigma, z, out):
         accs = {}
         out_sb = {}
 
-        def load_rows(pool, src, chunk, name):
-            rows = pool.tile([P, ROW_TILES * FEATURES], BF16, name=name, tag=name)
+        def load_rows(rows, src, group, chunks):
+            cols = slice(chunks.start * ROW_TILES * FEATURES, chunks.stop * ROW_TILES * FEATURES)
             nc.sync.dma_start(
-                out=rows[:],
-                in_=src[chunk * CHUNK : (chunk + 1) * CHUNK, :].rearrange(
-                    "(p j) k -> p (j k)", j=ROW_TILES
-                ),
+                out=rows[:, cols],
+                in_=src[group * GROUP * CHUNK : (group + 1) * GROUP * CHUNK, :].rearrange(
+                    "(p j) k -> p (j k)", j=GROUP * ROW_TILES
+                )[:, cols],
             )
-            return rows
+
+        def h_tile(group):
+            if group not in h_sb:
+                h_sb[group] = h_pool.tile([P, GROUP * ROW_TILES * FEATURES], BF16, name="h_rows", tag="h_rows")
+            return h_sb[group]
+
+        def z_tile(layer, group):
+            if (layer, group) not in z_sb:
+                z_sb[layer, group] = z_pool.tile(
+                    [P, GROUP * ROW_TILES * FEATURES], BF16, name="z_rows%d" % layer, tag="z_rows%d" % layer
+                )
+            return z_sb[layer, group]
 
         def load_h(chunk):
-            h_sb[chunk] = load_rows(h_pool, h_in, chunk, "h_rows")
+            load_rows(h_tile(chunk // GROUP), h_in, chunk // GROUP, range(chunk % GROUP, chunk % GROUP + 1))
 
         def load_z(unit):
-            z_sb[unit] = load_rows(z_pool, z[unit[1]], unit[0], "z_rows")
+            chunk, layer = unit
+            load_rows(z_tile(layer, chunk // GROUP), z[layer], chunk // GROUP, range(chunk % GROUP, chunk % GROUP + 1))
 
-        def load_unit(unit):
-            if unit[1] == 0:
-                load_h(unit[0])
-            load_z(unit)
+        def load_group(layer, group):
+            if layer == 0:
+                load_rows(h_tile(group), h_in, group, range(GROUP))
+            load_rows(z_tile(layer, group), z[layer], group, range(GROUP))
+
+        def words_of(rows, chunk, j, u):
+            start = ((chunk % GROUP) * ROW_TILES + j) * WORDS + u * P
+            return rows[:].bitcast(F32)[:, start : start + P]
 
         def load_weights(layer, u):
             if u == 0:
@@ -192,7 +209,6 @@ def tile_scm_mlp_pa_t_kernel(tc, h_in, w, masks, mu, sigma, z, out):
             )
 
         def transpose_h(chunk):
-            words = h_sb[chunk][:].bitcast(F32)
             grouped = h_group_pool.tile([P, CHUNK * PACK], BF16, name="h_grouped", tag="h_grouped", align_bytes=64)
             grouped_words = grouped[:].bitcast(F32).rearrange("p (c u) -> p c u", u=SIDES)
             for half in range(HALVES):
@@ -202,7 +218,7 @@ def tile_scm_mlp_pa_t_kernel(tc, h_in, w, masks, mu, sigma, z, out):
                     for u in range(SIDES):
                         nc.tensor.transpose(
                             h_t[:, u, jj * P : (jj + 1) * P],
-                            words[:, j * WORDS + u * P : j * WORDS + (u + 1) * P],
+                            words_of(h_sb[chunk // GROUP], chunk, j, u),
                             ident_f32[:],
                         )
                 nc.scalar.copy(
@@ -226,7 +242,6 @@ def tile_scm_mlp_pa_t_kernel(tc, h_in, w, masks, mu, sigma, z, out):
 
         def noise(unit, u):
             layer = unit[1]
-            words = z_sb[unit][:].bitcast(F32)
             if u == 0:
                 sums[unit] = sum_pool.tile([P, BLOCKS, CHUNK], F32, name="total", tag="total")
             total = sums[unit]
@@ -234,7 +249,7 @@ def tile_scm_mlp_pa_t_kernel(tc, h_in, w, masks, mu, sigma, z, out):
             for j in range(ROW_TILES):
                 nc.tensor.transpose(
                     z_t[:, j * P : (j + 1) * P],
-                    words[:, j * WORDS + u * P : j * WORDS + (u + 1) * P],
+                    words_of(z_sb[layer, unit[0] // GROUP], unit[0], j, u),
                     ident_f32[:],
                 )
             pairs = z_t[:].bitcast(BF16).rearrange("q (c e) -> q c e", e=PAIR)
@@ -296,7 +311,11 @@ def tile_scm_mlp_pa_t_kernel(tc, h_in, w, masks, mu, sigma, z, out):
                     nc.vector.tensor_scalar_max(out=dst, in0=src, scalar1=0.0)
                 else:
                     nc.scalar.activation(out=dst, in_=src, func=ACT.Relu)
-            dram = out[chunk * CHUNK : (chunk + 1) * CHUNK, :].rearrange("(p j) f -> p j f", j=ROW_TILES)
+            group = chunk // GROUP
+            first = (chunk % GROUP) * ROW_TILES
+            dram = out[group * GROUP * CHUNK : (group + 1) * GROUP * CHUNK, :].rearrange(
+                "(p j) f -> p j f", j=GROUP * ROW_TILES
+            )[:, first : first + ROW_TILES, :]
             if unit == units[-1]:
                 for j in range(PER_HALF * half, PER_HALF * (half + 1)):
                     nc.sync.dma_start(out=dram[:, j, features], in_=rows[:, j, features])
@@ -313,8 +332,10 @@ def tile_scm_mlp_pa_t_kernel(tc, h_in, w, masks, mu, sigma, z, out):
         load_h(units[1][0])
         load_weights(1, 0)
         load_weights(1, 1)
-        for i in range(2, LOAD_AHEAD):
-            load_unit(units[i])
+        load_z(units[2])
+        load_group(0, 1)
+        load_z(units[4])
+        load_group(1, 1)
 
         for u in range(SIDES):
             noise(units[0], u)
@@ -338,8 +359,11 @@ def tile_scm_mlp_pa_t_kernel(tc, h_in, w, masks, mu, sigma, z, out):
             return (0, 1, 3) if copies_h else (3,)
 
         for n in range(n_units + 1):
-            if unit_at(n + LOAD_AHEAD) is not None:
-                load_unit(unit_at(n + LOAD_AHEAD))
+            if unit_at(n + NOISE_AHEAD - 1) is not None:
+                chunk, layer = unit_at(n + NOISE_AHEAD - 1)
+                group = chunk // GROUP + LOAD_GROUPS
+                if chunk % GROUP == GROUP - 1 and group < GROUPS:
+                    load_group(layer, group)
             h_next = next_layer0(n + 1) if layer_at(n + 1) == 0 else None
             on_vector = relu_copies_on_vector(n, h_next is not None)
 

@@ -154,17 +154,23 @@ def tile_scm_mlp_pa_t_kernel(tc, h_in, w, masks, mu, sigma, z, out):
         ident_bf16 = const.tile([P, P], BF16)
         make_identity(nc, ident_bf16[:])
 
-        noise_scale = const.tile([P, LAYERS, BLOCKS], F32)
-        noise_bias = const.tile([P, LAYERS, BLOCKS], F32)
-        with nc.allow_non_contiguous_dma(reason="two small vectors, two features to a partition"):
-            for layer in range(LAYERS):
-                for src, dst, name in ((sigma, noise_scale, "sg%d"), (mu, noise_bias, "mu%d")):
-                    raw = const.tile([P, BLOCKS], BF16, name=name % layer)
-                    nc.scalar.dma_start(
-                        out=raw[:].rearrange("q (u e) -> q u e", e=PAIR),
-                        in_=src[layer].rearrange("(u q e) -> q u e", u=SIDES, e=PAIR),
-                    )
-                    nc.vector.tensor_copy(out=dst[:, layer, :], in_=raw[:])
+        vector_rows = {}
+        for name in ("sigma", "mu"):
+            vector_rows[name] = const.tile([P, SIDES * P], BF16, name=name + "_rows")
+            nc.vector.memset(vector_rows[name][:], 0.0)
+        noise_values = const.tile([P, 2, LAYERS * BLOCKS], F32)
+
+        def prepare_vectors():
+            v_t = psum_tr.tile([P, 2, P], F32, name="v_t", tag="tr")
+            for v, name in enumerate(("sigma", "mu")):
+                nc.tensor.transpose(v_t[:, v, :], vector_rows[name][:].bitcast(F32), ident_f32[:])
+            nc.vector.tensor_copy(
+                out=noise_values[:],
+                in_=v_t[:].rearrange("q v r -> q (v r)").bitcast(BF16).rearrange("q (v r) -> q v r", v=2)[
+                    :, :, 0 : LAYERS * BLOCKS
+                ],
+            )
+
         warm = const.tile([P, 1], F32)
         nc.scalar.activation(out=warm[:], in_=ident_f32[:, 0:1], func=ACT.Exp)
 
@@ -259,8 +265,8 @@ def tile_scm_mlp_pa_t_kernel(tc, h_in, w, masks, mu, sigma, z, out):
                     out=total[:, b, :],
                     in_=pairs[:, :, e],
                     func=ACT.Exp,
-                    bias=noise_bias[:, layer, b : b + 1],
-                    scale=noise_scale[:, layer, b : b + 1],
+                    bias=noise_values[:, 1, layer * BLOCKS + b : layer * BLOCKS + b + 1],
+                    scale=noise_values[:, 0, layer * BLOCKS + b : layer * BLOCKS + b + 1],
                 )
 
         def multiply_and_add(unit, half):
@@ -325,6 +331,10 @@ def tile_scm_mlp_pa_t_kernel(tc, h_in, w, masks, mu, sigma, z, out):
                 nc.sync.dma_start(out=dram[:, tiles, :], in_=rows[:, tiles, :])
 
         load_z(units[0])
+        for name, src in (("sigma", sigma), ("mu", mu)):
+            nc.sync.dma_start(
+                out=vector_rows[name][0 : LAYERS * SIDES, :], in_=src.rearrange("l (u k) -> (l u) k", u=SIDES)
+            )
         load_weights(0, 0)
         load_h(units[0][0])
         load_weights(0, 1)
@@ -337,6 +347,7 @@ def tile_scm_mlp_pa_t_kernel(tc, h_in, w, masks, mu, sigma, z, out):
         load_z(units[4])
         load_group(1, 1)
 
+        prepare_vectors()
         for u in range(SIDES):
             noise(units[0], u)
         transpose_h(units[0][0])

@@ -81,8 +81,8 @@ def tile_scm_mlp_pa_t_kernel(tc, h_in, w, masks, mu, sigma, z, out):
         a_group_pool = ctx.enter_context(tc.tile_pool(name="a_group_pool", bufs=A_GROUPED))
         code_pool = ctx.enter_context(tc.tile_pool(name="code_pool", bufs=CODE_TILES))
         out_pool = ctx.enter_context(tc.tile_pool(name="out_pool", bufs=OUT_TILES))
-        psum_pre = ctx.enter_context(tc.psum_pool(name="psum_pre", bufs=MX_BANKS))
-        psum_tr = ctx.enter_context(tc.psum_pool(name="psum_tr", bufs=TRANSPOSE_BANKS))
+        psum_all = ctx.enter_context(tc.psum_pool(name="psum_all", bufs=8))
+        psum_pre = psum_tr = psum_all
         ctx.enter_context(tc.manual_schedule())
 
         h_sb = {}
@@ -273,7 +273,7 @@ def tile_scm_mlp_pa_t_kernel(tc, h_in, w, masks, mu, sigma, z, out):
             layer = unit[1]
             total = sums[unit]
             for b in range(PER_HALF * half, PER_HALF * (half + 1)):
-                acc = psum_pre.tile([P, CHUNK], F32, name="acc", tag="acc")
+                acc = psum_pre.tile([P, CHUNK], F32, name="acc", tag="tr")
                 nc.tensor.matmul_mx(
                     out=acc[:],
                     lhsT=w_codes[layer][:, b * P : (b + 1) * P].bitcast(FP8X4),

from contextlib import ExitStack

import concourse.mybir as mybir
from concourse.masks import make_identity

FLOPS = 2 * 2 * 4096 * 512 * 512

F32 = mybir.dt.float32
BF16 = mybir.dt.bfloat16
U32 = mybir.dt.uint32
U8 = mybir.dt.uint8
FP8X4 = mybir.dt.float8_e4m3fn_x4
ACT = mybir.ActivationFunctionType
ALU = mybir.AluOpType

P = 128
PAIR = 2
SIDES = 2
PACK = SIDES * PAIR
FEATURES = P * PACK
WORDS = FEATURES // PAIR
LAYERS = 2
ROWS = 4096
CHUNK = 512
CHUNKS = ROWS // CHUNK
GROUP = 2
GROUPS = CHUNKS // GROUP
ROW_TILES = CHUNK // P
BLOCKS = FEATURES // P
HALVES = 2
PER_HALF = BLOCKS // HALVES
FLOAT_MAX = 3.4028234663852886e38

LAYER_LAG = 1
LOAD_GROUPS = 2
NOISE_AHEAD = 2

JOINED = range(0, 5)

MX_BANKS = 3
TRANSPOSE_BANKS = 5
SUM_TILES = 6
H_GROUPED = 2
A_GROUPED = 3
CODE_TILES = 3
OUT_TILES = 4


def unit_order():
    units = []
    for chunk in range(CHUNKS + LAYER_LAG):
        if chunk < CHUNKS:
            units.append((chunk, 0))
        if chunk >= LAYER_LAG:
            units.append((chunk - LAYER_LAG, 1))
    return units


def tile_scm_mlp_pa_t_kernel(tc, h_in, w, masks, mu, sigma, z, out):
    nc = tc.nc
    units = unit_order()
    n_units = len(units)

    def unit_at(i):
        return units[i] if 0 <= i < n_units else None

    def layer_at(i):
        return units[i][1] if 0 <= i < n_units else None

    def next_layer0(i):
        later = [m for m in range(i + 1, n_units) if units[m][1] == 0]
        return later[0] if later else None

    with ExitStack() as ctx:
        const = ctx.enter_context(tc.tile_pool(name="const", bufs=1))
        weights = ctx.enter_context(tc.tile_pool(name="weights", bufs=1))
        h_pool = ctx.enter_context(tc.tile_pool(name="h_pool", bufs=LOAD_GROUPS))
        z_pool = ctx.enter_context(tc.tile_pool(name="z_pool", bufs=LOAD_GROUPS))
        sum_pool = ctx.enter_context(tc.tile_pool(name="sum_pool", bufs=SUM_TILES))
        h_group_pool = ctx.enter_context(tc.tile_pool(name="h_group_pool", bufs=H_GROUPED))
        a_group_pool = ctx.enter_context(tc.tile_pool(name="a_group_pool", bufs=A_GROUPED))
        code_pool = ctx.enter_context(tc.tile_pool(name="code_pool", bufs=CODE_TILES))
        out_pool = ctx.enter_context(tc.tile_pool(name="out_pool", bufs=OUT_TILES))
        psum_all = ctx.enter_context(tc.psum_pool(name="psum_all", bufs=8))
        psum_pre = psum_tr = psum_all
        ctx.enter_context(tc.manual_schedule())

        h_sb = {}
        z_sb = {}
        w_sb = {}
        m_sb = {}
        w_grouped = {}
        w_codes = {}
        w_scales = {}
        h_grouped = {}
        a_grouped = {}
        x_codes = {}
        x_scales = {}
        sums = {}
        accs = {}
        out_sb = {}

        def load_rows(rows, src, group, chunks):
            cols = slice(chunks.start * ROW_TILES * FEATURES, chunks.stop * ROW_TILES * FEATURES)
            nc.sync.dma_start(
                out=rows[:, cols],
                in_=src[group * GROUP * CHUNK : (group + 1) * GROUP * CHUNK, :].rearrange(
                    "(p j) k -> p (j k)", j=GROUP * ROW_TILES
                )[:, cols],
            )

        def h_tile(group):
            if group not in h_sb:
                h_sb[group] = h_pool.tile([P, GROUP * ROW_TILES * FEATURES], BF16, name="h_rows", tag="h_rows")
            return h_sb[group]

        def z_tile(layer, group):
            if (layer, group) not in z_sb:
                z_sb[layer, group] = z_pool.tile(
                    [P, GROUP * ROW_TILES * FEATURES], BF16, name="z_rows%d" % layer, tag="z_rows%d" % layer
                )
            return z_sb[layer, group]

        def load_h(chunk):
            load_rows(h_tile(chunk // GROUP), h_in, chunk // GROUP, range(chunk % GROUP, chunk % GROUP + 1))

        def load_z(unit):
            chunk, layer = unit
            load_rows(z_tile(layer, chunk // GROUP), z[layer], chunk // GROUP, range(chunk % GROUP, chunk % GROUP + 1))

        def load_group(layer, group):
            if layer == 0:
                load_rows(h_tile(group), h_in, group, range(GROUP))
            load_rows(z_tile(layer, group), z[layer], group, range(GROUP))

        def words_of(rows, chunk, j, u):
            start = ((chunk % GROUP) * ROW_TILES + j) * WORDS + u * P
            return rows[:].bitcast(F32)[:, start : start + P]

        def load_weights(layer, u):
            if u == 0:
                w_sb[layer] = weights.tile([P, BLOCKS, FEATURES], BF16, name="w_raw%d" % layer)
                m_sb[layer] = weights.tile([P, BLOCKS, FEATURES], BF16, name="m_raw%d" % layer)
            for src, raw in ((w, w_sb[layer]), (masks, m_sb[layer])):
                nc.sync.dma_start(
                    out=raw[:, PAIR * u : PAIR * (u + 1), :].rearrange("q e k -> q (e k)"),
                    in_=src[layer][PAIR * u * P : PAIR * (u + 1) * P, :].rearrange(
                        "(q e) k -> q (e k)", e=PAIR
                    ),
                )

        ident_f32 = const.tile([P, P], F32)
        make_identity(nc, ident_f32[:])
        ident_bf16 = const.tile([P, P], BF16)
        make_identity(nc, ident_bf16[:])

        vector_rows = {}
        for name in ("sigma", "mu"):
            vector_rows[name] = const.tile([P, SIDES * P], BF16, name=name + "_rows")
            nc.vector.memset(vector_rows[name][:], 0.0)
        noise_values = const.tile([P, 2, LAYERS * BLOCKS], F32)

        def prepare_vectors():
            v_t = psum_tr.tile([P, 2, P], F32, name="v_t", tag="tr")
            for v, name in enumerate(("sigma", "mu")):
                nc.tensor.transpose(v_t[:, v, :], vector_rows[name][:].bitcast(F32), ident_f32[:])
            nc.vector.tensor_copy(
                out=noise_values[:],
                in_=v_t[:].rearrange("q v r -> q (v r)").bitcast(BF16).rearrange("q (v r) -> q v r", v=2)[
                    :, :, 0 : LAYERS * BLOCKS
                ],
            )

        warm = const.tile([P, 1], F32)
        nc.scalar.activation(out=warm[:], in_=ident_f32[:, 0:1], func=ACT.Exp)

        def mask_weights(layer, u):
            blocks = slice(PAIR * u, PAIR * (u + 1))
            nc.vector.tensor_tensor(
                out=w_sb[layer][:, blocks, :],
                in0=w_sb[layer][:, blocks, :],
                in1=m_sb[layer][:, blocks, :],
                op=ALU.mult,
            )

        def transpose_weights(layer, half, engine):
            if half == 0:
                w_grouped[layer] = weights.tile(
                    [P, FEATURES, PACK], BF16, name="w_grouped%d" % layer, align_bytes=64
                )
            w_t = psum_tr.tile([P, PER_HALF, PACK, P], BF16, name="w_t", tag="tr")
            for bb in range(PER_HALF):
                k_view = w_sb[layer][:, PER_HALF * half + bb, :].rearrange(
                    "q (u p e) -> q u e p", u=SIDES, e=PAIR
                )
                for t in range(PACK):
                    nc.tensor.transpose(w_t[:, bb, t, :], k_view[:, t // PAIR, t % PAIR, :], ident_bf16[:])
            dst = w_grouped[layer][:, PER_HALF * half * P : PER_HALF * (half + 1) * P, :].rearrange(
                "p (bb q) t -> p bb q t", bb=PER_HALF
            )
            if engine == "scalar":
                nc.scalar.copy(out=dst, in_=w_t[:].rearrange("p bb t q -> p bb q t"))
            else:
                nc.vector.tensor_copy(out=dst, in_=w_t[:].rearrange("p bb t q -> p bb q t"))

        def quantise_weights(layer, half):
            if half == 0:
                w_codes[layer] = weights.tile([P, FEATURES], U32, name="w_codes%d" % layer, align_bytes=64)
                w_scales[layer] = weights.tile([P, FEATURES], U8, name="w_scales%d" % layer, align_bytes=64)
            cols = slice(PER_HALF * half * P, PER_HALF * (half + 1) * P)
            nc.vector.quantize_mx(
                out=w_codes[layer][:, cols].bitcast(FP8X4),
                scales=w_scales[layer][:, cols],
                in_=w_grouped[layer][:, cols, :].rearrange("p c t -> p (c t)"),
            )

        def transpose_h(chunk):
            grouped = h_group_pool.tile([P, CHUNK * PACK], BF16, name="h_grouped", tag="h_grouped", align_bytes=64)
            grouped_words = grouped[:].bitcast(F32).rearrange("p (c u) -> p c u", u=SIDES)
            for half in range(HALVES):
                h_t = psum_tr.tile([P, SIDES, PER_HALF * P], F32, name="h_t", tag="tr")
                for jj in range(PER_HALF):
                    j = PER_HALF * half + jj
                    for u in range(SIDES):
                        nc.tensor.transpose(
                            h_t[:, u, jj * P : (jj + 1) * P],
                            words_of(h_sb[chunk // GROUP], chunk, j, u),
                            ident_f32[:],
                        )
                nc.scalar.copy(
                    out=grouped_words[:, PER_HALF * half * P : PER_HALF * (half + 1) * P, :],
                    in_=h_t[:].rearrange("p u c -> p c u"),
                )
            h_grouped[chunk] = grouped

        def quantise_moving(unit, grouped_flat, name):
            x_codes[unit] = code_pool.tile([P, CHUNK], U32, name=name + "_codes", tag=name + "_codes", align_bytes=64)
            x_scales[unit] = code_pool.tile([P, CHUNK], U8, name=name + "_scales", tag=name + "_scales", align_bytes=64)
            nc.vector.quantize_mx(
                out=x_codes[unit][:].bitcast(FP8X4), scales=x_scales[unit][:], in_=grouped_flat
            )

        def quantise_h(unit):
            quantise_moving(unit, h_grouped[unit[0]][:], "h")

        def quantise_a0(unit):
            quantise_moving(unit, a_grouped[unit[0]][:].rearrange("p c t -> p (c t)"), "a")

        def noise(unit, u):
            layer = unit[1]
            if u == 0:
                sums[unit] = sum_pool.tile([P, BLOCKS, CHUNK], F32, name="total", tag="total")
            total = sums[unit]
            z_t = psum_tr.tile([P, CHUNK], F32, name="z_t", tag="tr")
            for j in range(ROW_TILES):
                nc.tensor.transpose(
                    z_t[:, j * P : (j + 1) * P],
                    words_of(z_sb[layer, unit[0] // GROUP], unit[0], j, u),
                    ident_f32[:],
                )
            pairs = z_t[:].bitcast(BF16).rearrange("q (c e) -> q c e", e=PAIR)
            for e in range(PAIR):
                b = PAIR * u + e
                nc.scalar.activation(
                    out=total[:, b, :],
                    in_=pairs[:, :, e],
                    func=ACT.Exp,
                    bias=noise_values[:, 1, layer * BLOCKS + b : layer * BLOCKS + b + 1],
                    scale=noise_values[:, 0, layer * BLOCKS + b : layer * BLOCKS + b + 1],
                )

        def multiply_and_add(unit, half):
            layer = unit[1]
            total = sums[unit]
            for b in range(PER_HALF * half, PER_HALF * (half + 1)):
                acc = psum_pre.tile([P, CHUNK], F32, name="acc", tag="tr")
                nc.tensor.matmul_mx(
                    out=acc[:],
                    lhsT=w_codes[layer][:, b * P : (b + 1) * P].bitcast(FP8X4),
                    lhsT_scale=w_scales[layer][:, b * P : (b + 1) * P],
                    rhs=x_codes[unit][:].bitcast(FP8X4),
                    rhs_scale=x_scales[unit][:],
                    start=True,
                    stop=True,
                )
                accs[b] = acc
            for b in range(PER_HALF * half, PER_HALF * (half + 1)):
                nc.vector.tensor_tensor(out=total[:, b, :], in0=accs[b][:], in1=total[:, b, :], op=ALU.add)

        def regroup_a0(chunk):
            grouped = a_group_pool.tile([P, CHUNK, PACK], BF16, name="a_grouped", tag="a_grouped", align_bytes=64)
            nc.gpsimd.tensor_scalar(
                out=grouped[:],
                in0=sums[(chunk, 0)][:].rearrange("q b c -> q c b"),
                scalar1=FLOAT_MAX,
                scalar2=0.0,
                op0=ALU.min,
                op1=ALU.max,
            )
            a_grouped[chunk] = grouped

        def finish(unit, half, on_vector):
            chunk, layer = unit
            total = sums[unit]
            if half == 0 and layer == 0:
                out_sb[chunk] = out_pool.tile([P, ROW_TILES, LAYERS * FEATURES], F32, name="out_rows", tag="out_rows")
            rows = out_sb[chunk]
            features = slice(layer * FEATURES, (layer + 1) * FEATURES)
            tiles = slice(PER_HALF * half, PER_HALF * (half + 1))
            for j in range(PER_HALF * half, PER_HALF * (half + 1)):
                o_t = psum_tr.tile([P, BLOCKS, P], F32, name="o_t", tag="tr")
                for b in range(BLOCKS):
                    nc.tensor.transpose(o_t[:, b, :], total[:, b, j * P : (j + 1) * P], ident_f32[:])
                dst = rows[:, j, features].rearrange("p (u q e) -> p u q e", u=SIDES, e=PAIR)
                src = o_t[:].rearrange("p (u e) q -> p u q e", e=PAIR)
                if j in on_vector:
                    nc.vector.tensor_scalar_max(out=dst, in0=src, scalar1=0.0)
                else:
                    nc.scalar.activation(out=dst, in_=src, func=ACT.Relu)
            group = chunk // GROUP
            first = (chunk % GROUP) * ROW_TILES
            dram = out[group * GROUP * CHUNK : (group + 1) * GROUP * CHUNK, :].rearrange(
                "(p j) f -> p j f", j=GROUP * ROW_TILES
            )[:, first : first + ROW_TILES, :]
            if unit == units[-1]:
                for j in range(PER_HALF * half, PER_HALF * (half + 1)):
                    nc.sync.dma_start(out=dram[:, j, features], in_=rows[:, j, features])
            elif chunk not in JOINED:
                nc.sync.dma_start(out=dram[:, tiles, features], in_=rows[:, tiles, features])
            elif layer == LAYERS - 1:
                nc.sync.dma_start(out=dram[:, tiles, :], in_=rows[:, tiles, :])

        load_z(units[0])
        for name, src in (("sigma", sigma), ("mu", mu)):
            nc.sync.dma_start(
                out=vector_rows[name][0 : LAYERS * SIDES, :], in_=src.rearrange("l (u k) -> (l u) k", u=SIDES)
            )
        load_weights(0, 0)
        load_h(units[0][0])
        load_weights(0, 1)
        load_z(units[1])
        load_h(units[1][0])
        load_weights(1, 0)
        load_weights(1, 1)
        load_z(units[2])
        load_group(0, 1)
        load_z(units[4])
        load_group(1, 1)

        prepare_vectors()
        for u in range(SIDES):
            noise(units[0], u)
        transpose_h(units[0][0])
        for half in range(HALVES):
            mask_weights(0, half)
        for half in range(HALVES):
            transpose_weights(0, half, "vector")
        for half in range(HALVES):
            quantise_weights(0, half)
        quantise_h(units[0])
        for u in range(SIDES):
            noise(units[1], u)
        transpose_h(units[1][0])

        def relu_copies_on_vector(n, copies_h):
            if n == n_units:
                return (1, 3)
            if unit_at(n + NOISE_AHEAD) is None:
                return ()
            return (0, 1, 3) if copies_h else (3,)

        for n in range(n_units + 1):
            if unit_at(n + NOISE_AHEAD - 1) is not None:
                chunk, layer = unit_at(n + NOISE_AHEAD - 1)
                group = chunk // GROUP + LOAD_GROUPS
                if chunk % GROUP == GROUP - 1 and group < GROUPS:
                    load_group(layer, group)
            h_next = next_layer0(n + 1) if layer_at(n + 1) == 0 else None
            on_vector = relu_copies_on_vector(n, h_next is not None)

            for half in range(HALVES):
                if unit_at(n) is not None:
                    multiply_and_add(unit_at(n), half)
                    if half == HALVES - 1 and layer_at(n) == 0:
                        regroup_a0(unit_at(n)[0])
                if unit_at(n + NOISE_AHEAD) is not None:
                    noise(unit_at(n + NOISE_AHEAD), half)
                if unit_at(n - 1) is not None:
                    finish(unit_at(n - 1), half, on_vector)
                if half == 0:
                    if layer_at(n) == 0 and next_layer0(n) is not None:
                        quantise_h(units[next_layer0(n)])
                    if n == 0:
                        for u in range(SIDES):
                            mask_weights(1, u)
                    if n == 1:
                        for u in range(HALVES):
                            quantise_weights(1, u)
                    if layer_at(n + 1) == 1:
                        quantise_a0(unit_at(n + 1))
                    if h_next is not None and n > 0:
                        transpose_h(units[h_next][0])
                if n == 0 and half == HALVES - 1:
                    for u in range(HALVES):
                        transpose_weights(1, u, "scalar")
                    transpose_h(units[h_next][0])
